import numpy as np
import ml_dtypes


def mxq(x, axis, fmt="e4m3"):
    dtype, down = {"e4m3": (ml_dtypes.float8_e4m3fn, 7), "e5m2": (ml_dtypes.float8_e5m2, 14)}[fmt]
    v = np.moveaxis(np.asarray(x, np.float32).astype(ml_dtypes.bfloat16).astype(np.float64), axis, -1)
    blocks = v.reshape(v.shape[:-1] + (-1, 32))
    amax = np.abs(blocks).max(-1, keepdims=True)
    byte = np.maximum(np.where(amax > 0, np.frexp(amax)[1] - 1 + 127, 0) - down, 1)
    scale = np.exp2(byte - 127.0)
    codes = (blocks / scale).astype(np.float32).astype(dtype).astype(np.float64)
    return np.moveaxis((codes * scale).reshape(v.shape), -1, axis)


WIDE = False


def mx_kscale(k):
    if not WIDE:
        return np.ones(k)
    levels = np.array([10, -10, 5, -5, 0])
    a = np.random.permutation(np.resize(levels, k // 512 * 4)).reshape(k // 512, 4)
    idx = np.arange(k)
    return np.exp2(a[idx // 512, idx % 128 // 32])


BF16 = ml_dtypes.bfloat16


def bf(x):
    return np.asarray(x, np.float32).astype(BF16)


def f64(x):
    return np.asarray(x).astype(np.float64)


E2M1 = np.array([0.0, 0.5, 1.0, 1.5, 2.0, 3.0, 4.0, 6.0, -0.0, -0.5, -1.0, -1.5, -2.0, -3.0, -4.0, -6.0])


def pack_weight(w, fmt):
    k, n = w.shape
    w = f64(bf(w)).reshape(k // 32, 32, n)
    amax = np.abs(w).max(1)
    if fmt == "e4m3":
        byte = np.frexp(amax)[1] - 1 + 127 - 7
    else:
        mant, ex = np.frexp(amax / 6.0)
        byte = np.where(mant > 0.5, ex, ex - 1) + 127
    byte = np.clip(np.where(amax > 0, byte, 1), 1, 254)
    scaled = (w * np.exp2(127.0 - byte)[:, None, :]).reshape(k, n).astype(np.float32)
    by_word = np.ascontiguousarray(scaled.reshape(k // 512, 128, 4, n).transpose(0, 1, 3, 2))
    if fmt == "e4m3":
        words = by_word.astype(ml_dtypes.float8_e4m3fn).view(np.uint8)
    else:
        c = by_word.astype(ml_dtypes.float4_e2m1fn).view(np.uint8) & 0xF
        words = c[..., 0::2] | (c[..., 1::2] << 4)
    return np.ascontiguousarray(words), np.ascontiguousarray(byte.astype(np.uint8).reshape(k // 512, 16, n))


def unpack_weight(words, scales, fmt):
    g, p, n, _ = words.shape
    if fmt == "e4m3":
        vals = np.ascontiguousarray(words).view(ml_dtypes.float8_e4m3fn).astype(np.float64)
    else:
        nib = np.empty((g, p, n, 4), np.uint8)
        nib[..., 0::2] = words & 0xF
        nib[..., 1::2] = words >> 4
        vals = E2M1[nib]
    vals = vals * np.repeat(np.exp2(scales.astype(np.float64) - 127.0), 8, axis=1)[..., None]
    return vals.transpose(0, 1, 3, 2).reshape(g * 512, n)


M, K, N = 1024, 2048, 2048
TINY = 1e-15
EPS = 1e-6
C = 1.0
S = 1.0 / np.sqrt(C)
SQRTC = np.sqrt(C)


def _asinh(t):
    return np.log(t + np.sqrt(t * t + 1.0))


def _sinh(t):
    return 0.5 * (np.exp(t) - np.exp(-t))


def _norm(p):
    return np.sqrt(np.sum(p * p, axis=-1, keepdims=True))


def _sinhc(z):
    y = _sinh(z) / np.maximum(z, EPS)
    y0 = 1.0 + z * z / 6.0
    return np.where(np.abs(z) < EPS, y0, y)


def _beta(x):
    denom = np.sqrt(1.0 + C * np.sum(x * x, axis=-1, keepdims=True))
    return 1.0 / np.maximum(denom, TINY)


def _log0(y):
    s = _norm(y)
    coef = _asinh(s / S) / np.maximum(s / S, EPS)
    return coef * y


def _exp0(v):
    r = _norm(v)
    coef = _sinh(r / S) / np.maximum(r / S, EPS)
    return coef * v


def _proj_tan0(v, max_norm=20.0):
    r = np.maximum(_norm(v), EPS)
    return np.minimum(max_norm / r, 1.0) * v


def _pt_0_to_y(y, v):
    b = _beta(y)
    coef = C * b / (1.0 + b)
    dot = np.sum(y * v, axis=-1, keepdims=True)
    return v + coef * dot * y


def _gyro_add(x, y):
    b_x = _beta(x)
    b_y = _beta(y)
    s2 = S * S
    xy = np.sum(x * y, axis=-1, keepdims=True)
    coef = b_x / (1.0 + b_x) * (xy / s2) + (1.0 - b_y) / b_y
    return x + y + coef * x


def _exp_map(x, v):
    s2 = S * S
    x_norm2 = np.sum(x * x, axis=-1, keepdims=True)
    v_norm2 = np.sum(v * v, axis=-1, keepdims=True)
    dot_x_v = np.sum(x * v, axis=-1, keepdims=True)
    g_pvv = np.maximum(v_norm2 - dot_x_v * dot_x_v / (s2 + x_norm2), TINY)
    r_g = np.sqrt(g_pvv)
    b_x = _beta(x)
    coef1 = b_x / (1.0 + b_x)
    coef2 = -(C * b_x ** 3) / np.maximum(1.0 + b_x, TINY) ** 2
    dpi_v = coef1 * v + coef2 * dot_x_v * x
    lambda_x = (1.0 + b_x) / np.maximum(b_x, TINY)
    z_arg = np.clip(SQRTC * r_g, -20.0, 20.0)
    w = lambda_x * _sinhc(z_arg) * dpi_v
    return _gyro_add(x, w)


def setup_inputs():
    xn, un, bn = 3.0, 2.0, 2.0
    ax, aw, ab = 0.5, 2.0, 0.75
    s = mx_kscale(K)
    s = s / np.sqrt(np.mean(s * s))
    xs = xn / np.sqrt(K * (1.0 + ax * ax))
    ws = un / (_asinh(xn) * np.sqrt(N * (1.0 + ax * ax + ax * ax * aw * aw) / (1.0 + ax * ax)))
    bs = bn / np.sqrt(N * (1.0 + ab * ab))
    x = bf((np.random.standard_normal((M, K)) + ax) * xs * s)
    w_nk = (np.random.standard_normal((N, K)) + aw / np.sqrt(K)) * ws / s
    words, scales = pack_weight(np.ascontiguousarray(w_nk.T), "e4m3")
    b = bf((np.random.standard_normal(N) + ab) * bs)
    return {"x": x, "W_words": words, "W_scales": scales, "b": b}


def reference(x, W_words, W_scales, b):
    x, b = f64(x), f64(b)
    v = _log0(x)
    u = mxq(v, 1, "e4m3") @ unpack_weight(W_words, W_scales, "e4m3")
    u = _proj_tan0(u)
    y = _exp0(u)
    bt = _pt_0_to_y(y, b)
    return _exp_map(y, bt)

@@ -1,0 +1,317 @@
+from contextlib import ExitStack
+
+import concourse.mybir as mybir
+from concourse.masks import make_identity
+
+F32 = mybir.dt.float32
+BF16 = mybir.dt.bfloat16
+I32 = mybir.dt.int32
+U32 = mybir.dt.uint32
+U8 = mybir.dt.uint8
+FP8X4 = mybir.dt.float8_e4m3fn_x4
+ALU = mybir.AluOpType
+ACT = mybir.ActivationFunctionType
+AX = mybir.AxisListType
+
+P = 128
+M, K, N = 1024, 2048, 2048
+ROW_TILES = M // P
+PASSES = K // (4 * P)
+BANK = 512
+BANKS = N // BANK
+LEAD = 4
+EARLY = 2
+FLOPS = 2 * M * K * N
+
+EXP_20 = 485165195.4097903
+LOG2_E = 1.4426950408889634
+
+
+def tile_pvfc_kernel(tc, x, W_words, W_scales, b, out):
+    nc = tc.nc
+    with ExitStack() as ctx:
+        keep = ctx.enter_context(tc.tile_pool(name="keep", bufs=1))
+        work = ctx.enter_context(tc.tile_pool(name="work", bufs=2))
+        scrap = ctx.enter_context(tc.tile_pool(name="scrap", bufs=4))
+        small = ctx.enter_context(tc.tile_pool(name="small", bufs=3))
+        results = ctx.enter_context(tc.tile_pool(name="results", bufs=5))
+        psum_t = ctx.enter_context(tc.psum_pool(name="psum_t", bufs=2))
+        psum_short = ctx.enter_context(tc.psum_pool(name="psum_short", bufs=2))
+        psum_long = ctx.enter_context(tc.psum_pool(name="psum_long", bufs=4))
+
+        b_row = keep.tile([P, N], BF16)
+        nc.vector.memset(b_row[:], 0.0)
+        w_planes = keep.tile([P, N], U8, align_bytes=64)
+        nc.vector.memset(w_planes[:].bitcast(I32), 0)
+        ones = keep.tile([P, P], BF16)
+        nc.vector.memset(ones[:], 1.0)
+        exponents = keep.tile([P, 3], F32)
+        nc.vector.memset(exponents[:, 0:2], 0.5)
+        nc.vector.memset(exponents[:, 2:3], -0.5)
+        minus_one = keep.tile([P, 1], F32)
+        nc.vector.memset(minus_one[:], -1.0)
+        twos = keep.tile([P, 2], F32)
+        nc.vector.memset(twos[:, 0:1], 2.0)
+        nc.vector.memset(twos[:, 1:2], 0.5)
+        ident = keep.tile([P, P], F32)
+        make_identity(nc, ident[:])
+
+        nc.sync.dma_start(out=b_row[0:1, :], in_=b.rearrange("(o n) -> o n", o=1))
+        x_sb = []
+        for i in range(ROW_TILES):
+            x_sb.append(keep.tile([P, K], BF16, name="x%d" % i))
+        w_words = keep.tile([P, BANKS, PASSES, BANK], U32, align_bytes=64)
+        w_view = W_words.rearrange("g p n t -> p g (n t)").bitcast(I32)
+
+        def load_x(i):
+            nc.sync.dma_start(out=x_sb[i][:], in_=x[i * P : (i + 1) * P, :])
+
+        def load_w(j):
+            nc.sync.dma_start(
+                out=w_words[:, j, :, :].bitcast(I32),
+                in_=w_view[:, :, j * BANK : (j + 1) * BANK],
+            )
+
+        for i in range(4):
+            load_x(i)
+        for q in range(4):
+            nc.sync.dma_start(
+                out=w_planes[32 * q : 32 * q + 16, :].bitcast(I32),
+                in_=W_scales[:, 4 * q : 4 * q + 4, :].bitcast(I32),
+            )
+        for half in range(2):
+            load_w(2 * half)
+            load_w(2 * half + 1)
+            load_x(4 + 2 * half)
+            load_x(5 + 2 * half)
+
+        v_codes = keep.tile([P, ROW_TILES, PASSES * P], U32, align_bytes=64)
+        v_planes = keep.tile([P, ROW_TILES, PASSES * P], U8, align_bytes=64)
+
+        asinh = []
+        roots = []
+        for i in range(ROW_TILES):
+            squares = work.tile([P, K], BF16)
+            norm_in = keep.tile([P, 3], F32, name="norm_in%d" % i)
+            nc.scalar.activation(
+                out=squares[:], in_=x_sb[i][:], func=ACT.Square, accum_out=norm_in[:, 0:1]
+            )
+            nc.gpsimd.tensor_scalar_add(norm_in[:, 1:2], norm_in[:, 0:1], 1.0)
+            nc.gpsimd.tensor_scalar_max(norm_in[:, 2:3], norm_in[:, 0:1], 1e-12)
+            root = keep.tile([P, 3], F32, name="root%d" % i)
+            nc.gpsimd.tensor_tensor(out=root[:], in0=norm_in[:], in1=exponents[:], op=ALU.pow)
+            log = keep.tile([P, 1], F32, name="asinh%d" % i)
+            nc.scalar.activation(
+                out=log[:], in_=root[:, 0:1], func=ACT.Ln, bias=root[:, 1:2], scale=1.0
+            )
+            asinh.append(log)
+            roots.append(root)
+
+        b_bc = keep.tile([P, N], BF16)
+        bb4 = keep.tile([P, BANKS], F32)
+        for j in range(BANKS):
+            cols = slice(j * BANK, (j + 1) * BANK)
+            bank = psum_long.tile([P, BANK], F32, name="bank", tag="bank")
+            nc.tensor.matmul(bank[:], lhsT=ones[:], rhs=b_row[:, cols], start=True, stop=True)
+            nc.vector.tensor_copy(out=b_bc[:, cols], in_=bank[:])
+            product = scrap.tile([P, BANK], F32)
+            nc.vector.scalar_tensor_tensor(
+                out=product[:], in0=bank[:], scalar=1.0, in1=b_bc[:, cols],
+                op0=ALU.mult, op1=ALU.mult, accum_out=bb4[:, j : j + 1],
+            )
+        sc_half = keep.tile([P, 1], F32)
+        cw_half = keep.tile([P, 1], F32)
+        sc_b = keep.tile([P, N], F32)
+
+        def numbers_of_b():
+            bb = keep.tile([P, 1], F32)
+            nc.vector.reduce_sum(out=bb[:], in_=bb4[:], axis=AX.X)
+            z = keep.tile([P, 1], F32)
+            nc.gpsimd.tensor_scalar_max(z[:], bb[:], 1e-15)
+            nc.gpsimd.tensor_tensor(out=z[:], in0=z[:], in1=exponents[:, 0:1], op=ALU.pow)
+            nc.gpsimd.tensor_scalar_min(z[:], z[:], 20.0)
+            z_log2e = keep.tile([P, 1], F32)
+            nc.gpsimd.tensor_scalar_mul(z_log2e[:], z[:], LOG2_E)
+            exps = keep.tile([P, 2], F32)
+            nc.gpsimd.tensor_tensor(
+                out=exps[:], in0=twos[:], in1=z_log2e[:].to_broadcast([P, 2]), op=ALU.pow
+            )
+            inv_z = keep.tile([P, 1], F32)
+            nc.gpsimd.tensor_scalar_max(inv_z[:], z[:], 1e-6)
+            nc.gpsimd.tensor_tensor(out=inv_z[:], in0=inv_z[:], in1=minus_one[:], op=ALU.pow)
+            sc_big = keep.tile([P, 1], F32)
+            nc.gpsimd.tensor_sub(sc_big[:], exps[:, 0:1], exps[:, 1:2])
+            nc.gpsimd.tensor_scalar(
+                out=sc_big[:], in0=sc_big[:], scalar1=inv_z[:], scalar2=0.5,
+                op0=ALU.mult, op1=ALU.mult,
+            )
+            sc_small = keep.tile([P, 1], F32)
+            nc.gpsimd.tensor_mul(sc_small[:], z[:], z[:])
+            nc.gpsimd.tensor_scalar(
+                out=sc_small[:], in0=sc_small[:], scalar1=1.0 / 6.0, scalar2=1.0,
+                op0=ALU.mult, op1=ALU.add,
+            )
+            is_small = keep.tile([P, 1], F32)
+            nc.gpsimd.tensor_single_scalar(is_small[:], z[:], 1e-6, op=ALU.is_lt)
+            sc = keep.tile([P, 1], F32)
+            nc.gpsimd.tensor_sub(sc_small[:], sc_small[:], sc_big[:])
+            nc.gpsimd.tensor_scalar(
+                out=sc[:], in0=sc_small[:], scalar1=is_small[:], scalar2=sc_big[:],
+                op0=ALU.mult, op1=ALU.add,
+            )
+            cw = keep.tile([P, 1], F32)
+            nc.gpsimd.tensor_scalar(
+                out=cw[:], in0=sc[:], scalar1=sc[:], scalar2=bb[:], op0=ALU.mult, op1=ALU.mult
+            )
+            nc.gpsimd.tensor_scalar_add(cw[:], cw[:], 1.0)
+            nc.gpsimd.tensor_tensor(out=cw[:], in0=cw[:], in1=exponents[:, 0:1], op=ALU.pow)
+            nc.gpsimd.tensor_scalar_mul(cw_half[:], cw[:], 0.5)
+            nc.gpsimd.tensor_scalar_mul(sc_half[:], sc[:], 0.5)
+            nc.gpsimd.tensor_scalar(
+                out=sc_b[:], in0=b_bc[:], scalar1=sc[:], scalar2=1.0, op0=ALU.mult, op1=ALU.mult
+            )
+
+        def quantise_rows(i):
+            v_sb = work.tile([P, K], BF16)
+            nc.vector.tensor_scalar(
+                out=v_sb[:], in0=x_sb[i][:], scalar1=asinh[i][:], scalar2=roots[i][:, 2:3],
+                op0=ALU.mult, op1=ALU.mult,
+            )
+            v_pairs = v_sb[:].bitcast(F32)
+            grouped = work.tile([P, K], BF16, align_bytes=64)
+            grouped_pairs = grouped[:].bitcast(F32).rearrange(
+                "p (g m u) -> p g m u", g=PASSES, u=2
+            )
+            for h in range(2):
+                flipped = psum_t.tile([P, 2, 2, P], F32)
+                for gg in range(2):
+                    g = 2 * h + gg
+                    for u in range(2):
+                        nc.tensor.transpose(
+                            flipped[:, gg, u, :],
+                            v_pairs[:, 256 * g + u : 256 * (g + 1) : 2],
+                            ident[:],
+                        )
+                nc.vector.tensor_copy(
+                    out=grouped_pairs[:, 2 * h : 2 * h + 2, :, :],
+                    in_=flipped[:].rearrange("p g u m -> p g m u"),
+                )
+            nc.vector.quantize_mx(
+                out=v_codes[:, i, :].bitcast(FP8X4), scales=v_planes[:, i, :], in_=grouped[:]
+            )
+
+        def multiply(i):
+            late_banks = []
+            sq4 = small.tile([P, BANKS], F32)
+            dot4 = small.tile([P, BANKS], F32)
+            result = results.tile([P, N], F32)
+            for j in range(BANKS):
+                cols = slice(j * BANK, (j + 1) * BANK)
+                if j < EARLY:
+                    bank = psum_short.tile([P, BANK], F32, name="early", tag="early")
+                else:
+                    bank = psum_long.tile([P, BANK], F32, name="bank", tag="bank")
+                    late_banks.append(bank)
+                for g in range(PASSES):
+                    rows = slice(g * P, (g + 1) * P)
+                    nc.tensor.matmul_mx(
+                        out=bank[:],
+                        lhsT=v_codes[:, i, rows].bitcast(FP8X4),
+                        lhsT_scale=v_planes[:, i, rows],
+                        rhs=w_words[:, j, g, :].bitcast(FP8X4),
+                        rhs_scale=w_planes[4 * g : P, cols],
+                        start=(g == 0),
+                        stop=(g == PASSES - 1),
+                    )
+                square = scrap.tile([P, BANK], BF16)
+                nc.scalar.activation(
+                    out=square[:], in_=bank[:], func=ACT.Square, accum_out=sq4[:, j : j + 1]
+                )
+                if j < EARLY:
+                    nc.scalar.copy(out=result[:, cols], in_=bank[:])
+                    u0 = result[:, cols]
+                else:
+                    u0 = bank[:]
+                product = scrap.tile([P, BANK], F32)
+                nc.vector.scalar_tensor_tensor(
+                    out=product[:], in0=u0, scalar=1.0, in1=b_bc[:, cols],
+                    op0=ALU.mult, op1=ALU.mult, accum_out=dot4[:, j : j + 1],
+                )
+            return late_banks, sq4, dot4, result
+
+        def finish(i, late_banks, sq4, dot4, result):
+            norm2 = small.tile([P, 2], F32)
+            nc.vector.reduce_sum(out=norm2[:, 0:1], in_=sq4[:], axis=AX.X)
+            nc.vector.tensor_scalar_max(norm2[:, 1:2], norm2[:, 0:1], 1e-12)
+            norm = small.tile([P, 2], F32)
+            nc.gpsimd.tensor_tensor(
+                out=norm[:], in0=norm2[:], in1=exponents[:, 1:3], op=ALU.pow
+            )
+            exp_r = small.tile([P, 1], F32)
+            exp_mr = small.tile([P, 1], F32)
+            tanh_half = small.tile([P, 1], F32)
+            nc.scalar.activation(out=tanh_half[:], in_=norm[:, 0:1], func=ACT.Tanh, scale=0.5)
+            nc.scalar.activation(out=exp_mr[:], in_=norm[:, 0:1], func=ACT.Exp, scale=-1.0)
+            nc.scalar.activation(out=exp_r[:], in_=norm[:, 0:1], func=ACT.Exp)
+            dot = small.tile([P, 1], F32)
+            nc.vector.reduce_sum(out=dot[:], in_=dot4[:], axis=AX.X)
+            nc.vector.scalar_tensor_tensor(
+                out=dot[:], in0=dot[:], scalar=sc_half[:], in1=norm[:, 1:2],
+                op0=ALU.mult, op1=ALU.mult,
+            )
+            bracket = small.tile([P, 1], F32)
+            nc.vector.tensor_scalar(
+                out=bracket[:], in0=tanh_half[:], scalar1=dot[:], scalar2=cw_half[:],
+                op0=ALU.mult, op1=ALU.add,
+            )
+            sinh2 = small.tile([P, 1], F32)
+            nc.vector.scalar_tensor_tensor(
+                out=sinh2[:], in0=exp_r[:], scalar=EXP_20, in1=exp_mr[:],
+                op0=ALU.min, op1=ALU.subtract,
+            )
+            gain = small.tile([P, 1], F32)
+            nc.vector.scalar_tensor_tensor(
+                out=gain[:], in0=sinh2[:], scalar=norm[:, 1:2], in1=bracket[:],
+                op0=ALU.mult, op1=ALU.mult,
+            )
+            rows = slice(i * P, (i + 1) * P)
+            for j in range(EARLY, BANKS):
+                cols = slice(j * BANK, (j + 1) * BANK)
+                nc.vector.scalar_tensor_tensor(
+                    out=result[:, cols], in0=late_banks[j - EARLY][:], scalar=gain[:],
+                    in1=sc_b[:, cols], op0=ALU.mult, op1=ALU.add,
+                )
+            late = slice(EARLY * BANK, N)
+            nc.sync.dma_start(out=out[rows, late], in_=result[:, late])
+            return gain
+
+        def finish_early(i, result, gain):
+            rows = slice(i * P, (i + 1) * P)
+            early = slice(0, EARLY * BANK)
+            if i < ROW_TILES - 1:
+                nc.gpsimd.tensor_scalar(
+                    out=result[:, early], in0=result[:, early], scalar1=gain[:], scalar2=1.0,
+                    op0=ALU.mult, op1=ALU.mult,
+                )
+                nc.gpsimd.tensor_tensor(
+                    out=result[:, early], in0=result[:, early], in1=sc_b[:, early], op=ALU.add
+                )
+            else:
+                nc.vector.scalar_tensor_tensor(
+                    out=result[:, early], in0=result[:, early], scalar=gain[:],
+                    in1=sc_b[:, early], op0=ALU.mult, op1=ALU.add,
+                )
+            nc.sync.dma_start(out=out[rows, early], in_=result[:, early])
+
+        numbers_of_b()
+        for i in range(LEAD):
+            quantise_rows(i)
+        products = multiply(0)
+        for i in range(ROW_TILES):
+            if i + LEAD < ROW_TILES:
+                quantise_rows(i + LEAD)
+            gain = finish(i, *products)
+            result = products[3]
+            if i + 1 < ROW_TILES:
+                products = multiply(i + 1)
+            finish_early(i, result, gain)

@@ -288,19 +288,10 @@ def tile_pvfc_kernel(tc, x, W_words, W_scales, b, out):
         def finish_early(i, result, gain):
             rows = slice(i * P, (i + 1) * P)
             early = slice(0, EARLY * BANK)
-            if i < ROW_TILES - 1:
-                nc.gpsimd.tensor_scalar(
-                    out=result[:, early], in0=result[:, early], scalar1=gain[:], scalar2=1.0,
-                    op0=ALU.mult, op1=ALU.mult,
-                )
-                nc.gpsimd.tensor_tensor(
-                    out=result[:, early], in0=result[:, early], in1=sc_b[:, early], op=ALU.add
-                )
-            else:
-                nc.vector.scalar_tensor_tensor(
-                    out=result[:, early], in0=result[:, early], scalar=gain[:],
-                    in1=sc_b[:, early], op0=ALU.mult, op1=ALU.add,
-                )
+            nc.vector.scalar_tensor_tensor(
+                out=result[:, early], in0=result[:, early], scalar=gain[:],
+                in1=sc_b[:, early], op0=ALU.mult, op1=ALU.add,
+            )
             nc.sync.dma_start(out=out[rows, early], in_=result[:, early])
 
         numbers_of_b()

@@ -19,8 +19,8 @@ ROW_TILES = M // P
 PASSES = K // (4 * P)
 BANK = 512
 BANKS = N // BANK
-LEAD = 4
 EARLY = 2
+LEAD = 5
 FLOPS = 2 * M * K * N
 
 EXP_20 = 485165195.4097903
@@ -30,14 +30,15 @@ LOG2_E = 1.4426950408889634
 def tile_pvfc_kernel(tc, x, W_words, W_scales, b, out):
     nc = tc.nc
     with ExitStack() as ctx:
+        ctx.enter_context(tc.manual_schedule())
         keep = ctx.enter_context(tc.tile_pool(name="keep", bufs=1))
         work = ctx.enter_context(tc.tile_pool(name="work", bufs=2))
         scrap = ctx.enter_context(tc.tile_pool(name="scrap", bufs=4))
         small = ctx.enter_context(tc.tile_pool(name="small", bufs=3))
-        results = ctx.enter_context(tc.tile_pool(name="results", bufs=5))
+        results = ctx.enter_context(tc.tile_pool(name="results", bufs=4))
         psum_t = ctx.enter_context(tc.psum_pool(name="psum_t", bufs=2))
-        psum_short = ctx.enter_context(tc.psum_pool(name="psum_short", bufs=2))
-        psum_long = ctx.enter_context(tc.psum_pool(name="psum_long", bufs=4))
+        psum_early = ctx.enter_context(tc.psum_pool(name="psum_early", bufs=2))
+        psum_late = ctx.enter_context(tc.psum_pool(name="psum_late", bufs=4))
 
         b_row = keep.tile([P, N], BF16)
         nc.vector.memset(b_row[:], 0.0)
@@ -55,42 +56,35 @@ def tile_pvfc_kernel(tc, x, W_words, W_scales, b, out):
         nc.vector.memset(twos[:, 1:2], 0.5)
         ident = keep.tile([P, P], F32)
         make_identity(nc, ident[:])
+        warm = keep.tile([P, 1], F32)
+        nc.scalar.activation(out=warm[:], in_=twos[:, 0:1], func=ACT.Ln)
 
         nc.sync.dma_start(out=b_row[0:1, :], in_=b.rearrange("(o n) -> o n", o=1))
         x_sb = []
         for i in range(ROW_TILES):
-            x_sb.append(keep.tile([P, K], BF16, name="x%d" % i))
-        w_words = keep.tile([P, BANKS, PASSES, BANK], U32, align_bytes=64)
-        w_view = W_words.rearrange("g p n t -> p g (n t)").bitcast(I32)
-
-        def load_x(i):
-            nc.sync.dma_start(out=x_sb[i][:], in_=x[i * P : (i + 1) * P, :])
-
-        def load_w(j):
-            nc.sync.dma_start(
-                out=w_words[:, j, :, :].bitcast(I32),
-                in_=w_view[:, :, j * BANK : (j + 1) * BANK],
-            )
-
-        for i in range(4):
-            load_x(i)
+            x_tile = keep.tile([P, K], BF16, name="x%d" % i)
+            nc.sync.dma_start(out=x_tile[:], in_=x[i * P : (i + 1) * P, :])
+            x_sb.append(x_tile)
         for q in range(4):
             nc.sync.dma_start(
                 out=w_planes[32 * q : 32 * q + 16, :].bitcast(I32),
                 in_=W_scales[:, 4 * q : 4 * q + 4, :].bitcast(I32),
             )
-        for half in range(2):
-            load_w(2 * half)
-            load_w(2 * half + 1)
-            load_x(4 + 2 * half)
-            load_x(5 + 2 * half)
+        w_words = keep.tile([P, BANKS, PASSES, BANK], U32, align_bytes=64)
+        w_view = W_words.rearrange("g p n t -> p g (n t)").bitcast(I32)
+        for j in range(BANKS):
+            nc.sync.dma_start(
+                out=w_words[:, j, :, :].bitcast(I32),
+                in_=w_view[:, :, j * BANK : (j + 1) * BANK],
+            )
 
         v_codes = keep.tile([P, ROW_TILES, PASSES * P], U32, align_bytes=64)
         v_planes = keep.tile([P, ROW_TILES, PASSES * P], U8, align_bytes=64)
 
-        asinh = []
         roots = []
-        for i in range(ROW_TILES):
+        asinh = []
+
+        def square_sum(i):
             squares = work.tile([P, K], BF16)
             norm_in = keep.tile([P, 3], F32, name="norm_in%d" % i)
             nc.scalar.activation(
@@ -100,118 +94,136 @@ def tile_pvfc_kernel(tc, x, W_words, W_scales, b, out):
             nc.gpsimd.tensor_scalar_max(norm_in[:, 2:3], norm_in[:, 0:1], 1e-12)
             root = keep.tile([P, 3], F32, name="root%d" % i)
             nc.gpsimd.tensor_tensor(out=root[:], in0=norm_in[:], in1=exponents[:], op=ALU.pow)
+            roots.append(root)
+
+        def logarithm(i):
             log = keep.tile([P, 1], F32, name="asinh%d" % i)
             nc.scalar.activation(
-                out=log[:], in_=root[:, 0:1], func=ACT.Ln, bias=root[:, 1:2], scale=1.0
+                out=log[:], in_=roots[i][:, 0:1], func=ACT.Ln, bias=roots[i][:, 1:2], scale=1.0
             )
             asinh.append(log)
-            roots.append(root)
+
+        square_sum(0)
+        for i in range(1, ROW_TILES):
+            square_sum(i)
+            logarithm(i - 1)
+        logarithm(ROW_TILES - 1)
 
         b_bc = keep.tile([P, N], BF16)
         bb4 = keep.tile([P, BANKS], F32)
         for j in range(BANKS):
             cols = slice(j * BANK, (j + 1) * BANK)
-            bank = psum_long.tile([P, BANK], F32, name="bank", tag="bank")
+            bank = psum_late.tile([P, BANK], F32, name="late", tag="late")
             nc.tensor.matmul(bank[:], lhsT=ones[:], rhs=b_row[:, cols], start=True, stop=True)
             nc.vector.tensor_copy(out=b_bc[:, cols], in_=bank[:])
-            product = scrap.tile([P, BANK], F32)
+            product = scrap.tile([P, EARLY * BANK], F32)
             nc.vector.scalar_tensor_tensor(
-                out=product[:], in0=bank[:], scalar=1.0, in1=b_bc[:, cols],
+                out=product[:, 0:BANK], in0=bank[:], scalar=1.0, in1=b_bc[:, cols],
                 op0=ALU.mult, op1=ALU.mult, accum_out=bb4[:, j : j + 1],
             )
-        sc_half = keep.tile([P, 1], F32)
+        bb = keep.tile([P, 1], F32)
+        nc.vector.reduce_sum(out=bb[:], in_=bb4[:], axis=AX.X)
+        z = keep.tile([P, 1], F32)
+        nc.gpsimd.tensor_scalar_max(z[:], bb[:], 1e-15)
+        nc.gpsimd.tensor_tensor(out=z[:], in0=z[:], in1=exponents[:, 0:1], op=ALU.pow)
+        nc.gpsimd.tensor_scalar_min(z[:], z[:], 20.0)
+        z_log2e = keep.tile([P, 1], F32)
+        nc.gpsimd.tensor_scalar_mul(z_log2e[:], z[:], LOG2_E)
+        exps = keep.tile([P, 2], F32)
+        nc.gpsimd.tensor_tensor(
+            out=exps[:], in0=twos[:], in1=z_log2e[:].to_broadcast([P, 2]), op=ALU.pow
+        )
+        inv_z = keep.tile([P, 1], F32)
+        nc.gpsimd.tensor_scalar_max(inv_z[:], z[:], 1e-6)
+        nc.gpsimd.tensor_tensor(out=inv_z[:], in0=inv_z[:], in1=minus_one[:], op=ALU.pow)
+        sc_big = keep.tile([P, 1], F32)
+        nc.gpsimd.tensor_sub(sc_big[:], exps[:, 0:1], exps[:, 1:2])
+        nc.gpsimd.tensor_scalar(
+            out=sc_big[:], in0=sc_big[:], scalar1=inv_z[:], scalar2=0.5,
+            op0=ALU.mult, op1=ALU.mult,
+        )
+        sc_small = keep.tile([P, 1], F32)
+        nc.gpsimd.tensor_mul(sc_small[:], z[:], z[:])
+        nc.gpsimd.tensor_scalar(
+            out=sc_small[:], in0=sc_small[:], scalar1=1.0 / 6.0, scalar2=1.0,
+            op0=ALU.mult, op1=ALU.add,
+        )
+        is_small = keep.tile([P, 1], F32)
+        nc.gpsimd.tensor_single_scalar(is_small[:], z[:], 1e-6, op=ALU.is_lt)
+        sc = keep.tile([P, 1], F32)
+        nc.gpsimd.tensor_sub(sc_small[:], sc_small[:], sc_big[:])
+        nc.gpsimd.tensor_scalar(
+            out=sc[:], in0=sc_small[:], scalar1=is_small[:], scalar2=sc_big[:],
+            op0=ALU.mult, op1=ALU.add,
+        )
+        cw = keep.tile([P, 1], F32)
+        nc.gpsimd.tensor_scalar(
+            out=cw[:], in0=sc[:], scalar1=sc[:], scalar2=bb[:], op0=ALU.mult, op1=ALU.mult
+        )
+        nc.gpsimd.tensor_scalar_add(cw[:], cw[:], 1.0)
+        nc.gpsimd.tensor_tensor(out=cw[:], in0=cw[:], in1=exponents[:, 0:1], op=ALU.pow)
         cw_half = keep.tile([P, 1], F32)
+        sc_half = keep.tile([P, 1], F32)
+        nc.gpsimd.tensor_scalar_mul(cw_half[:], cw[:], 0.5)
+        nc.gpsimd.tensor_scalar_mul(sc_half[:], sc[:], 0.5)
         sc_b = keep.tile([P, N], F32)
+        nc.gpsimd.tensor_scalar(
+            out=sc_b[:], in0=b_bc[:], scalar1=sc[:], scalar2=1.0, op0=ALU.mult, op1=ALU.mult
+        )
 
-        def numbers_of_b():
-            bb = keep.tile([P, 1], F32)
-            nc.vector.reduce_sum(out=bb[:], in_=bb4[:], axis=AX.X)
-            z = keep.tile([P, 1], F32)
-            nc.gpsimd.tensor_scalar_max(z[:], bb[:], 1e-15)
-            nc.gpsimd.tensor_tensor(out=z[:], in0=z[:], in1=exponents[:, 0:1], op=ALU.pow)
-            nc.gpsimd.tensor_scalar_min(z[:], z[:], 20.0)
-            z_log2e = keep.tile([P, 1], F32)
-            nc.gpsimd.tensor_scalar_mul(z_log2e[:], z[:], LOG2_E)
-            exps = keep.tile([P, 2], F32)
-            nc.gpsimd.tensor_tensor(
-                out=exps[:], in0=twos[:], in1=z_log2e[:].to_broadcast([P, 2]), op=ALU.pow
-            )
-            inv_z = keep.tile([P, 1], F32)
-            nc.gpsimd.tensor_scalar_max(inv_z[:], z[:], 1e-6)
-            nc.gpsimd.tensor_tensor(out=inv_z[:], in0=inv_z[:], in1=minus_one[:], op=ALU.pow)
-            sc_big = keep.tile([P, 1], F32)
-            nc.gpsimd.tensor_sub(sc_big[:], exps[:, 0:1], exps[:, 1:2])
-            nc.gpsimd.tensor_scalar(
-                out=sc_big[:], in0=sc_big[:], scalar1=inv_z[:], scalar2=0.5,
-                op0=ALU.mult, op1=ALU.mult,
-            )
-            sc_small = keep.tile([P, 1], F32)
-            nc.gpsimd.tensor_mul(sc_small[:], z[:], z[:])
-            nc.gpsimd.tensor_scalar(
-                out=sc_small[:], in0=sc_small[:], scalar1=1.0 / 6.0, scalar2=1.0,
-                op0=ALU.mult, op1=ALU.add,
-            )
-            is_small = keep.tile([P, 1], F32)
-            nc.gpsimd.tensor_single_scalar(is_small[:], z[:], 1e-6, op=ALU.is_lt)
-            sc = keep.tile([P, 1], F32)
-            nc.gpsimd.tensor_sub(sc_small[:], sc_small[:], sc_big[:])
-            nc.gpsimd.tensor_scalar(
-                out=sc[:], in0=sc_small[:], scalar1=is_small[:], scalar2=sc_big[:],
-                op0=ALU.mult, op1=ALU.add,
-            )
-            cw = keep.tile([P, 1], F32)
-            nc.gpsimd.tensor_scalar(
-                out=cw[:], in0=sc[:], scalar1=sc[:], scalar2=bb[:], op0=ALU.mult, op1=ALU.mult
-            )
-            nc.gpsimd.tensor_scalar_add(cw[:], cw[:], 1.0)
-            nc.gpsimd.tensor_tensor(out=cw[:], in0=cw[:], in1=exponents[:, 0:1], op=ALU.pow)
-            nc.gpsimd.tensor_scalar_mul(cw_half[:], cw[:], 0.5)
-            nc.gpsimd.tensor_scalar_mul(sc_half[:], sc[:], 0.5)
-            nc.gpsimd.tensor_scalar(
-                out=sc_b[:], in0=b_bc[:], scalar1=sc[:], scalar2=1.0, op0=ALU.mult, op1=ALU.mult
-            )
+        v_tiles = {}
 
-        def quantise_rows(i):
+        def scale_rows(k):
             v_sb = work.tile([P, K], BF16)
             nc.vector.tensor_scalar(
-                out=v_sb[:], in0=x_sb[i][:], scalar1=asinh[i][:], scalar2=roots[i][:, 2:3],
+                out=v_sb[:], in0=x_sb[k][:], scalar1=asinh[k][:], scalar2=roots[k][:, 2:3],
                 op0=ALU.mult, op1=ALU.mult,
             )
-            v_pairs = v_sb[:].bitcast(F32)
+            v_tiles[k] = v_sb
+
+        def quantise_rows(k):
+            v_pairs = v_tiles[k][:].bitcast(F32)
+            flipped = []
+            for h in range(2):
+                bank = psum_t.tile([P, 2, 2, P], F32, name="flipped", tag="flipped")
+                for gg in range(2):
+                    g = 2 * h + gg
+                    for u in range(2):
+                        nc.tensor.transpose(
+                            bank[:, gg, u, :], v_pairs[:, 256 * g + u : 256 * (g + 1) : 2], ident[:]
+                        )
+                flipped.append(bank)
             grouped = work.tile([P, K], BF16, align_bytes=64)
             grouped_pairs = grouped[:].bitcast(F32).rearrange(
                 "p (g m u) -> p g m u", g=PASSES, u=2
             )
             for h in range(2):
-                flipped = psum_t.tile([P, 2, 2, P], F32)
-                for gg in range(2):
-                    g = 2 * h + gg
-                    for u in range(2):
-                        nc.tensor.transpose(
-                            flipped[:, gg, u, :],
-                            v_pairs[:, 256 * g + u : 256 * (g + 1) : 2],
-                            ident[:],
-                        )
                 nc.vector.tensor_copy(
                     out=grouped_pairs[:, 2 * h : 2 * h + 2, :, :],
-                    in_=flipped[:].rearrange("p g u m -> p g m u"),
+                    in_=flipped[h][:].rearrange("p g u m -> p g m u"),
                 )
+            if k + 1 < ROW_TILES:
+                scale_rows(k + 1)
             nc.vector.quantize_mx(
-                out=v_codes[:, i, :].bitcast(FP8X4), scales=v_planes[:, i, :], in_=grouped[:]
+                out=v_codes[:, k, :].bitcast(FP8X4), scales=v_planes[:, k, :], in_=grouped[:]
             )
 
+        banks = {}
+        result = {}
+        square_sums = {}
+        dot_sums = {}
+        norms = {}
+        dot_terms = {}
+        gains = {}
+
         def multiply(i):
-            late_banks = []
-            sq4 = small.tile([P, BANKS], F32)
-            dot4 = small.tile([P, BANKS], F32)
-            result = results.tile([P, N], F32)
+            banks[i] = []
             for j in range(BANKS):
                 cols = slice(j * BANK, (j + 1) * BANK)
                 if j < EARLY:
-                    bank = psum_short.tile([P, BANK], F32, name="early", tag="early")
+                    bank = psum_early.tile([P, BANK], F32, name="early", tag="early")
                 else:
-                    bank = psum_long.tile([P, BANK], F32, name="bank", tag="bank")
-                    late_banks.append(bank)
+                    bank = psum_late.tile([P, BANK], F32, name="late", tag="late")
                 for g in range(PASSES):
                     rows = slice(g * P, (g + 1) * P)
                     nc.tensor.matmul_mx(
@@ -223,86 +235,112 @@ def tile_pvfc_kernel(tc, x, W_words, W_scales, b, out):
                         start=(g == 0),
                         stop=(g == PASSES - 1),
                     )
-                square = scrap.tile([P, BANK], BF16)
-                nc.scalar.activation(
-                    out=square[:], in_=bank[:], func=ACT.Square, accum_out=sq4[:, j : j + 1]
-                )
-                if j < EARLY:
-                    nc.scalar.copy(out=result[:, cols], in_=bank[:])
-                    u0 = result[:, cols]
-                else:
-                    u0 = bank[:]
-                product = scrap.tile([P, BANK], F32)
-                nc.vector.scalar_tensor_tensor(
-                    out=product[:], in0=u0, scalar=1.0, in1=b_bc[:, cols],
-                    op0=ALU.mult, op1=ALU.mult, accum_out=dot4[:, j : j + 1],
-                )
-            return late_banks, sq4, dot4, result
+                banks[i].append(bank)
 
-        def finish(i, late_banks, sq4, dot4, result):
+        def square_sum_of_bank(i, j):
+            square = scrap.tile([P, BANK], BF16)
+            nc.scalar.activation(
+                out=square[:], in_=banks[i][j][:], func=ACT.Square,
+                accum_out=square_sums[i][:, j : j + 1],
+            )
+
+        def sums_early(i):
+            square_sums[i] = small.tile([P, BANKS], F32, name="square_sums", tag="square_sums")
+            dot_sums[i] = small.tile([P, BANKS - EARLY + 1], F32, name="dot_sums", tag="dot_sums")
+            result[i] = results.tile([P, N], F32, name="result", tag="result")
+            for j in range(EARLY):
+                square_sum_of_bank(i, j)
+                nc.scalar.copy(out=result[i][:, j * BANK : (j + 1) * BANK], in_=banks[i][j][:])
+            early = slice(0, EARLY * BANK)
+            product = scrap.tile([P, EARLY * BANK], F32)
+            nc.vector.scalar_tensor_tensor(
+                out=product[:], in0=result[i][:, early], scalar=1.0, in1=b_bc[:, early],
+                op0=ALU.mult, op1=ALU.mult, accum_out=dot_sums[i][:, 0:1],
+            )
+
+        def sums_late(i):
+            for j in range(EARLY, BANKS):
+                square_sum_of_bank(i, j)
+                product = scrap.tile([P, EARLY * BANK], F32)
+                nc.vector.scalar_tensor_tensor(
+                    out=product[:, 0:BANK], in0=banks[i][j][:], scalar=1.0,
+                    in1=b_bc[:, j * BANK : (j + 1) * BANK], op0=ALU.mult, op1=ALU.mult,
+                    accum_out=dot_sums[i][:, j - EARLY + 1 : j - EARLY + 2],
+                )
+
+        def start_gain(i):
             norm2 = small.tile([P, 2], F32)
-            nc.vector.reduce_sum(out=norm2[:, 0:1], in_=sq4[:], axis=AX.X)
-            nc.vector.tensor_scalar_max(norm2[:, 1:2], norm2[:, 0:1], 1e-12)
+            nc.vector.reduce_sum(out=norm2[:, 0:1], in_=square_sums[i][:], axis=AX.X)
+            dot = small.tile([P, 1], F32)
+            nc.vector.reduce_sum(out=dot[:], in_=dot_sums[i][:], axis=AX.X)
+            nc.gpsimd.tensor_scalar_max(norm2[:, 1:2], norm2[:, 0:1], 1e-12)
             norm = small.tile([P, 2], F32)
             nc.gpsimd.tensor_tensor(
                 out=norm[:], in0=norm2[:], in1=exponents[:, 1:3], op=ALU.pow
             )
-            exp_r = small.tile([P, 1], F32)
-            exp_mr = small.tile([P, 1], F32)
+            dot_term = small.tile([P, 1], F32)
+            nc.gpsimd.tensor_scalar(
+                out=dot_term[:], in0=dot[:], scalar1=sc_half[:], scalar2=norm[:, 1:2],
+                op0=ALU.mult, op1=ALU.mult,
+            )
+            norms[i] = norm
+            dot_terms[i] = dot_term
+
+        def end_gain(i):
+            norm = norms[i]
             tanh_half = small.tile([P, 1], F32)
+            exp_mr = small.tile([P, 1], F32)
+            exp_r = small.tile([P, 1], F32)
             nc.scalar.activation(out=tanh_half[:], in_=norm[:, 0:1], func=ACT.Tanh, scale=0.5)
             nc.scalar.activation(out=exp_mr[:], in_=norm[:, 0:1], func=ACT.Exp, scale=-1.0)
             nc.scalar.activation(out=exp_r[:], in_=norm[:, 0:1], func=ACT.Exp)
-            dot = small.tile([P, 1], F32)
-            nc.vector.reduce_sum(out=dot[:], in_=dot4[:], axis=AX.X)
-            nc.vector.scalar_tensor_tensor(
-                out=dot[:], in0=dot[:], scalar=sc_half[:], in1=norm[:, 1:2],
-                op0=ALU.mult, op1=ALU.mult,
-            )
             bracket = small.tile([P, 1], F32)
-            nc.vector.tensor_scalar(
-                out=bracket[:], in0=tanh_half[:], scalar1=dot[:], scalar2=cw_half[:],
+            nc.gpsimd.tensor_scalar(
+                out=bracket[:], in0=tanh_half[:], scalar1=dot_terms[i][:], scalar2=cw_half[:],
                 op0=ALU.mult, op1=ALU.add,
             )
             sinh2 = small.tile([P, 1], F32)
-            nc.vector.scalar_tensor_tensor(
-                out=sinh2[:], in0=exp_r[:], scalar=EXP_20, in1=exp_mr[:],
+            nc.gpsimd.tensor_scalar(
+                out=sinh2[:], in0=exp_r[:], scalar1=EXP_20, scalar2=exp_mr[:],
                 op0=ALU.min, op1=ALU.subtract,
             )
             gain = small.tile([P, 1], F32)
-            nc.vector.scalar_tensor_tensor(
-                out=gain[:], in0=sinh2[:], scalar=norm[:, 1:2], in1=bracket[:],
+            nc.gpsimd.tensor_scalar(
+                out=gain[:], in0=sinh2[:], scalar1=norm[:, 1:2], scalar2=bracket[:],
                 op0=ALU.mult, op1=ALU.mult,
             )
+            gains[i] = gain
+
+        def finish(i):
             rows = slice(i * P, (i + 1) * P)
             for j in range(EARLY, BANKS):
                 cols = slice(j * BANK, (j + 1) * BANK)
                 nc.vector.scalar_tensor_tensor(
-                    out=result[:, cols], in0=late_banks[j - EARLY][:], scalar=gain[:],
+                    out=result[i][:, cols], in0=banks[i][j][:], scalar=gains[i][:],
                     in1=sc_b[:, cols], op0=ALU.mult, op1=ALU.add,
                 )
             late = slice(EARLY * BANK, N)
-            nc.sync.dma_start(out=out[rows, late], in_=result[:, late])
-            return gain
-
-        def finish_early(i, result, gain):
-            rows = slice(i * P, (i + 1) * P)
+            nc.sync.dma_start(out=out[rows, late], in_=result[i][:, late])
             early = slice(0, EARLY * BANK)
             nc.vector.scalar_tensor_tensor(
-                out=result[:, early], in0=result[:, early], scalar=gain[:],
+                out=result[i][:, early], in0=result[i][:, early], scalar=gains[i][:],
                 in1=sc_b[:, early], op0=ALU.mult, op1=ALU.add,
             )
-            nc.sync.dma_start(out=out[rows, early], in_=result[:, early])
+            nc.sync.dma_start(out=out[rows, early], in_=result[i][:, early])
 
-        numbers_of_b()
-        for i in range(LEAD):
-            quantise_rows(i)
-        products = multiply(0)
-        for i in range(ROW_TILES):
+        scale_rows(0)
+        for k in range(LEAD):
+            quantise_rows(k)
+        for i in range(ROW_TILES + 1):
+            if i < ROW_TILES:
+                multiply(i)
+                sums_early(i)
+            if i > 0:
+                end_gain(i - 1)
+            if i < ROW_TILES:
+                sums_late(i)
+                start_gain(i)
             if i + LEAD < ROW_TILES:
                 quantise_rows(i + LEAD)
-            gain = finish(i, *products)
-            result = products[3]
-            if i + 1 < ROW_TILES:
-                products = multiply(i + 1)
-            finish_early(i, result, gain)
+            if i > 0:
+                finish(i - 1)

@@ -20,11 +20,11 @@ PASSES = K // (4 * P)
 BANK = 512
 BANKS = N // BANK
 EARLY = 2
-LEAD = 5
+LEAD = ROW_TILES - 2
 FLOPS = 2 * M * K * N
 
-EXP_20 = 485165195.4097903
 LOG2_E = 1.4426950408889634
+HUGE = 3.0e38
 
 
 def tile_pvfc_kernel(tc, x, W_words, W_scales, b, out):
@@ -40,31 +40,40 @@ def tile_pvfc_kernel(tc, x, W_words, W_scales, b, out):
         psum_early = ctx.enter_context(tc.psum_pool(name="psum_early", bufs=2))
         psum_late = ctx.enter_context(tc.psum_pool(name="psum_late", bufs=4))
 
+        def constant(name, values):
+            tile = keep.tile([P, len(values)], F32, name=name)
+            for c, value in enumerate(values):
+                nc.vector.memset(tile[:, c : c + 1], value)
+            return tile
+
         b_row = keep.tile([P, N], BF16)
-        nc.vector.memset(b_row[:], 0.0)
+        nc.vector.memset(b_row[:].bitcast(I32), 0)
         w_planes = keep.tile([P, N], U8, align_bytes=64)
         nc.vector.memset(w_planes[:].bitcast(I32), 0)
         ones = keep.tile([P, P], BF16)
         nc.vector.memset(ones[:], 1.0)
-        exponents = keep.tile([P, 3], F32)
-        nc.vector.memset(exponents[:, 0:2], 0.5)
-        nc.vector.memset(exponents[:, 2:3], -0.5)
-        minus_one = keep.tile([P, 1], F32)
-        nc.vector.memset(minus_one[:], -1.0)
-        twos = keep.tile([P, 2], F32)
-        nc.vector.memset(twos[:, 0:1], 2.0)
-        nc.vector.memset(twos[:, 1:2], 0.5)
+        twos = constant("twos", [2.0, 0.5])
+        exponents = constant("exponents", [0.5, 0.5, -0.5])
+        b_floor = constant("b_floor", [1e-15, 1e-12])
+        b_cap = constant("b_cap", [400.0, 400.0])
+        x_step = constant("x_step", [0.0, 1.0, 0.0])
+        x_floor = constant("x_floor", [0.0, 0.0, 1e-12])
+        u_cap = constant("u_cap", [400.0, HUGE])
+        u_floor = constant("u_floor", [0.0, 1e-12])
         ident = keep.tile([P, P], F32)
         make_identity(nc, ident[:])
         warm = keep.tile([P, 1], F32)
         nc.scalar.activation(out=warm[:], in_=twos[:, 0:1], func=ACT.Ln)
 
-        nc.sync.dma_start(out=b_row[0:1, :], in_=b.rearrange("(o n) -> o n", o=1))
         x_sb = []
         for i in range(ROW_TILES):
-            x_tile = keep.tile([P, K], BF16, name="x%d" % i)
-            nc.sync.dma_start(out=x_tile[:], in_=x[i * P : (i + 1) * P, :])
-            x_sb.append(x_tile)
+            x_sb.append(keep.tile([P, K], BF16, name="x%d" % i))
+        b_cols = keep.tile([P, N // P], BF16)
+        nc.sync.dma_start(out=x_sb[0][:], in_=x[0:P, :])
+        nc.sync.dma_start(out=b_cols[:], in_=b.rearrange("(p c) -> p c", p=P))
+        nc.sync.dma_start(out=b_row[0:1, :], in_=b.rearrange("(o n) -> o n", o=1))
+        for i in range(1, ROW_TILES):
+            nc.sync.dma_start(out=x_sb[i][:], in_=x[i * P : (i + 1) * P, :])
         for q in range(4):
             nc.sync.dma_start(
                 out=w_planes[32 * q : 32 * q + 16, :].bitcast(I32),
@@ -81,105 +90,43 @@ def tile_pvfc_kernel(tc, x, W_words, W_scales, b, out):
         v_codes = keep.tile([P, ROW_TILES, PASSES * P], U32, align_bytes=64)
         v_planes = keep.tile([P, ROW_TILES, PASSES * P], U8, align_bytes=64)
 
-        roots = []
-        asinh = []
+        x_sums = {}
+        x_roots = {}
+        asinh = {}
 
         def square_sum(i):
             squares = work.tile([P, K], BF16)
-            norm_in = keep.tile([P, 3], F32, name="norm_in%d" % i)
+            x_sums[i] = keep.tile([P, 1], F32, name="x_sum%d" % i)
             nc.scalar.activation(
-                out=squares[:], in_=x_sb[i][:], func=ACT.Square, accum_out=norm_in[:, 0:1]
+                out=squares[:], in_=x_sb[i][:], func=ACT.Square, accum_out=x_sums[i][:]
             )
-            nc.gpsimd.tensor_scalar_add(norm_in[:, 1:2], norm_in[:, 0:1], 1.0)
-            nc.gpsimd.tensor_scalar_max(norm_in[:, 2:3], norm_in[:, 0:1], 1e-12)
-            root = keep.tile([P, 3], F32, name="root%d" % i)
-            nc.gpsimd.tensor_tensor(out=root[:], in0=norm_in[:], in1=exponents[:], op=ALU.pow)
-            roots.append(root)
+
+        def roots(i):
+            radicands = keep.tile([P, 3], F32, name="radicands%d" % i)
+            nc.vector.scalar_tensor_tensor(
+                out=radicands[:], in0=x_step[:], scalar=x_sums[i][:], in1=x_floor[:],
+                op0=ALU.add, op1=ALU.max,
+            )
+            x_roots[i] = keep.tile([P, 3], F32, name="x_roots%d" % i)
+            nc.gpsimd.tensor_tensor(
+                out=x_roots[i][:], in0=radicands[:], in1=exponents[:], op=ALU.pow
+            )
 
         def logarithm(i):
-            log = keep.tile([P, 1], F32, name="asinh%d" % i)
+            asinh[i] = keep.tile([P, 1], F32, name="asinh%d" % i)
             nc.scalar.activation(
-                out=log[:], in_=roots[i][:, 0:1], func=ACT.Ln, bias=roots[i][:, 1:2], scale=1.0
+                out=asinh[i][:], in_=x_roots[i][:, 0:1], func=ACT.Ln,
+                bias=x_roots[i][:, 1:2], scale=1.0,
             )
-            asinh.append(log)
-
-        square_sum(0)
-        for i in range(1, ROW_TILES):
-            square_sum(i)
-            logarithm(i - 1)
-        logarithm(ROW_TILES - 1)
-
-        b_bc = keep.tile([P, N], BF16)
-        bb4 = keep.tile([P, BANKS], F32)
-        for j in range(BANKS):
-            cols = slice(j * BANK, (j + 1) * BANK)
-            bank = psum_late.tile([P, BANK], F32, name="late", tag="late")
-            nc.tensor.matmul(bank[:], lhsT=ones[:], rhs=b_row[:, cols], start=True, stop=True)
-            nc.vector.tensor_copy(out=b_bc[:, cols], in_=bank[:])
-            product = scrap.tile([P, EARLY * BANK], F32)
-            nc.vector.scalar_tensor_tensor(
-                out=product[:, 0:BANK], in0=bank[:], scalar=1.0, in1=b_bc[:, cols],
-                op0=ALU.mult, op1=ALU.mult, accum_out=bb4[:, j : j + 1],
-            )
-        bb = keep.tile([P, 1], F32)
-        nc.vector.reduce_sum(out=bb[:], in_=bb4[:], axis=AX.X)
-        z = keep.tile([P, 1], F32)
-        nc.gpsimd.tensor_scalar_max(z[:], bb[:], 1e-15)
-        nc.gpsimd.tensor_tensor(out=z[:], in0=z[:], in1=exponents[:, 0:1], op=ALU.pow)
-        nc.gpsimd.tensor_scalar_min(z[:], z[:], 20.0)
-        z_log2e = keep.tile([P, 1], F32)
-        nc.gpsimd.tensor_scalar_mul(z_log2e[:], z[:], LOG2_E)
-        exps = keep.tile([P, 2], F32)
-        nc.gpsimd.tensor_tensor(
-            out=exps[:], in0=twos[:], in1=z_log2e[:].to_broadcast([P, 2]), op=ALU.pow
-        )
-        inv_z = keep.tile([P, 1], F32)
-        nc.gpsimd.tensor_scalar_max(inv_z[:], z[:], 1e-6)
-        nc.gpsimd.tensor_tensor(out=inv_z[:], in0=inv_z[:], in1=minus_one[:], op=ALU.pow)
-        sc_big = keep.tile([P, 1], F32)
-        nc.gpsimd.tensor_sub(sc_big[:], exps[:, 0:1], exps[:, 1:2])
-        nc.gpsimd.tensor_scalar(
-            out=sc_big[:], in0=sc_big[:], scalar1=inv_z[:], scalar2=0.5,
-            op0=ALU.mult, op1=ALU.mult,
-        )
-        sc_small = keep.tile([P, 1], F32)
-        nc.gpsimd.tensor_mul(sc_small[:], z[:], z[:])
-        nc.gpsimd.tensor_scalar(
-            out=sc_small[:], in0=sc_small[:], scalar1=1.0 / 6.0, scalar2=1.0,
-            op0=ALU.mult, op1=ALU.add,
-        )
-        is_small = keep.tile([P, 1], F32)
-        nc.gpsimd.tensor_single_scalar(is_small[:], z[:], 1e-6, op=ALU.is_lt)
-        sc = keep.tile([P, 1], F32)
-        nc.gpsimd.tensor_sub(sc_small[:], sc_small[:], sc_big[:])
-        nc.gpsimd.tensor_scalar(
-            out=sc[:], in0=sc_small[:], scalar1=is_small[:], scalar2=sc_big[:],
-            op0=ALU.mult, op1=ALU.add,
-        )
-        cw = keep.tile([P, 1], F32)
-        nc.gpsimd.tensor_scalar(
-            out=cw[:], in0=sc[:], scalar1=sc[:], scalar2=bb[:], op0=ALU.mult, op1=ALU.mult
-        )
-        nc.gpsimd.tensor_scalar_add(cw[:], cw[:], 1.0)
-        nc.gpsimd.tensor_tensor(out=cw[:], in0=cw[:], in1=exponents[:, 0:1], op=ALU.pow)
-        cw_half = keep.tile([P, 1], F32)
-        sc_half = keep.tile([P, 1], F32)
-        nc.gpsimd.tensor_scalar_mul(cw_half[:], cw[:], 0.5)
-        nc.gpsimd.tensor_scalar_mul(sc_half[:], sc[:], 0.5)
-        sc_b = keep.tile([P, N], F32)
-        nc.gpsimd.tensor_scalar(
-            out=sc_b[:], in0=b_bc[:], scalar1=sc[:], scalar2=1.0, op0=ALU.mult, op1=ALU.mult
-        )
 
         v_tiles = {}
 
         def scale_rows(k):
-            v_sb = work.tile([P, K], BF16)
+            v_tiles[k] = work.tile([P, K], BF16, name="v_sb", tag="v_sb")
             nc.vector.tensor_scalar(
-                out=v_sb[:], in0=x_sb[k][:], scalar1=asinh[k][:], scalar2=roots[k][:, 2:3],
-                op0=ALU.mult, op1=ALU.mult,
+                out=v_tiles[k][:], in0=x_sb[k][:], scalar1=asinh[k][:],
+                scalar2=x_roots[k][:, 2:3], op0=ALU.mult, op1=ALU.mult,
             )
-            v_tiles[k] = v_sb
 
         def quantise_rows(k):
             v_pairs = v_tiles[k][:].bitcast(F32)
@@ -208,12 +155,87 @@ def tile_pvfc_kernel(tc, x, W_words, W_scales, b, out):
                 out=v_codes[:, k, :].bitcast(FP8X4), scales=v_planes[:, k, :], in_=grouped[:]
             )
 
+        square_sum(0)
+        square_sum(1)
+
+        b_squares = keep.tile([P, N // P], F32)
+        b_partial = keep.tile([P, 1], F32)
+        nc.vector.scalar_tensor_tensor(
+            out=b_squares[:], in0=b_cols[:], scalar=1.0, in1=b_cols[:],
+            op0=ALU.mult, op1=ALU.mult, accum_out=b_partial[:],
+        )
+        b_repeated = keep.tile([P, P], F32)
+        nc.vector.tensor_copy(out=b_repeated[:], in_=b_partial[:].to_broadcast([P, P]))
+        b_flipped = psum_t.tile([P, 2, 2, P], F32, name="flipped", tag="flipped")
+        nc.tensor.transpose(b_flipped[:, 0, 0, :], b_repeated[:], ident[:])
+        bb = keep.tile([P, 1], F32)
+        nc.vector.reduce_sum(out=bb[:], in_=b_flipped[:, 0, 0, :], axis=AX.X)
+
+        b_banks = []
+        for j in range(BANKS):
+            bank = psum_late.tile([P, BANK], F32, name="late", tag="late")
+            nc.tensor.matmul(
+                bank[:], lhsT=ones[:], rhs=b_row[:, j * BANK : (j + 1) * BANK],
+                start=True, stop=True,
+            )
+            b_banks.append(bank)
+        b_bc = keep.tile([P, N], BF16)
+
+        def copy_b(j):
+            nc.vector.tensor_copy(out=b_bc[:, j * BANK : (j + 1) * BANK], in_=b_banks[j][:])
+
+        z_radicands = keep.tile([P, 2], F32)
+        nc.vector.scalar_tensor_tensor(
+            out=z_radicands[:], in0=b_floor[:], scalar=bb[:], in1=b_cap[:],
+            op0=ALU.max, op1=ALU.min,
+        )
+        z_roots = keep.tile([P, 2], F32)
+        nc.gpsimd.tensor_tensor(
+            out=z_roots[:], in0=z_radicands[:], in1=exponents[:, 1:3], op=ALU.pow
+        )
+        copy_b(0)
+        copy_b(1)
+        z_log2e = keep.tile([P, 2], F32)
+        nc.vector.tensor_scalar_mul(z_log2e[:], z_roots[:, 0:1].to_broadcast([P, 2]), LOG2_E)
+        z_exps = keep.tile([P, 2], F32)
+        nc.gpsimd.tensor_tensor(out=z_exps[:], in0=twos[:], in1=z_log2e[:], op=ALU.pow)
+        copy_b(2)
+        copy_b(3)
+        roots(0)
+        logarithm(0)
+        sc_twice = keep.tile([P, 1], F32)
+        nc.vector.tensor_sub(sc_twice[:], z_exps[:, 0:1], z_exps[:, 1:2])
+        nc.vector.tensor_scalar(
+            out=sc_twice[:], in0=sc_twice[:], scalar1=z_roots[:, 1:2], scalar2=2.0,
+            op0=ALU.mult, op1=ALU.max,
+        )
+        sc_half = keep.tile([P, 1], F32)
+        nc.vector.tensor_scalar_mul(sc_half[:], sc_twice[:], 0.25)
+        cw_radicand = keep.tile([P, 1], F32)
+        nc.vector.tensor_mul(cw_radicand[:], sc_half[:], sc_half[:])
+        nc.vector.tensor_scalar(
+            out=cw_radicand[:], in0=cw_radicand[:], scalar1=bb[:], scalar2=0.25,
+            op0=ALU.mult, op1=ALU.add,
+        )
+        cw_half = keep.tile([P, 1], F32)
+        nc.gpsimd.tensor_tensor(
+            out=cw_half[:], in0=cw_radicand[:], in1=exponents[:, 0:1], op=ALU.pow
+        )
+        sc_b = keep.tile([P, N], F32)
+        nc.vector.tensor_scalar(
+            out=sc_b[:], in0=b_bc[:], scalar1=sc_twice[:], scalar2=0.5,
+            op0=ALU.mult, op1=ALU.mult,
+        )
+        scale_rows(0)
+        roots(1)
+
         banks = {}
         result = {}
         square_sums = {}
         dot_sums = {}
+        dots = {}
         norms = {}
-        dot_terms = {}
+        parts = {}
         gains = {}
 
         def multiply(i):
@@ -258,58 +280,65 @@ def tile_pvfc_kernel(tc, x, W_words, W_scales, b, out):
                 op0=ALU.mult, op1=ALU.mult, accum_out=dot_sums[i][:, 0:1],
             )
 
-        def sums_late(i):
-            for j in range(EARLY, BANKS):
-                square_sum_of_bank(i, j)
-                product = scrap.tile([P, EARLY * BANK], F32)
-                nc.vector.scalar_tensor_tensor(
-                    out=product[:, 0:BANK], in0=banks[i][j][:], scalar=1.0,
-                    in1=b_bc[:, j * BANK : (j + 1) * BANK], op0=ALU.mult, op1=ALU.mult,
-                    accum_out=dot_sums[i][:, j - EARLY + 1 : j - EARLY + 2],
-                )
+        def sums_late(i, j):
+            square_sum_of_bank(i, j)
+            product = scrap.tile([P, EARLY * BANK], F32)
+            nc.vector.scalar_tensor_tensor(
+                out=product[:, 0:BANK], in0=banks[i][j][:], scalar=1.0,
+                in1=b_bc[:, j * BANK : (j + 1) * BANK], op0=ALU.mult, op1=ALU.mult,
+                accum_out=dot_sums[i][:, j - EARLY + 1 : j - EARLY + 2],
+            )
 
-        def start_gain(i):
-            norm2 = small.tile([P, 2], F32)
-            nc.vector.reduce_sum(out=norm2[:, 0:1], in_=square_sums[i][:], axis=AX.X)
-            dot = small.tile([P, 1], F32)
-            nc.vector.reduce_sum(out=dot[:], in_=dot_sums[i][:], axis=AX.X)
-            nc.gpsimd.tensor_scalar_max(norm2[:, 1:2], norm2[:, 0:1], 1e-12)
-            norm = small.tile([P, 2], F32)
+        def norm_of(i):
+            u_sum = small.tile([P, 1], F32)
+            nc.vector.reduce_sum(out=u_sum[:], in_=square_sums[i][:], axis=AX.X)
+            dots[i] = small.tile([P, 1], F32, name="dot", tag="dot")
+            nc.vector.reduce_sum(out=dots[i][:], in_=dot_sums[i][:], axis=AX.X)
+            radicands = small.tile([P, 2], F32)
+            nc.vector.scalar_tensor_tensor(
+                out=radicands[:], in0=u_cap[:], scalar=u_sum[:], in1=u_floor[:],
+                op0=ALU.min, op1=ALU.max,
+            )
+            norms[i] = small.tile([P, 2], F32, name="norm", tag="norm")
             nc.gpsimd.tensor_tensor(
-                out=norm[:], in0=norm2[:], in1=exponents[:, 1:3], op=ALU.pow
+                out=norms[i][:], in0=radicands[:], in1=exponents[:, 1:3], op=ALU.pow
             )
-            dot_term = small.tile([P, 1], F32)
-            nc.gpsimd.tensor_scalar(
-                out=dot_term[:], in0=dot[:], scalar1=sc_half[:], scalar2=norm[:, 1:2],
-                op0=ALU.mult, op1=ALU.mult,
-            )
-            norms[i] = norm
-            dot_terms[i] = dot_term
 
-        def end_gain(i):
-            norm = norms[i]
-            tanh_half = small.tile([P, 1], F32)
-            exp_mr = small.tile([P, 1], F32)
-            exp_r = small.tile([P, 1], F32)
-            nc.scalar.activation(out=tanh_half[:], in_=norm[:, 0:1], func=ACT.Tanh, scale=0.5)
-            nc.scalar.activation(out=exp_mr[:], in_=norm[:, 0:1], func=ACT.Exp, scale=-1.0)
-            nc.scalar.activation(out=exp_r[:], in_=norm[:, 0:1], func=ACT.Exp)
-            bracket = small.tile([P, 1], F32)
-            nc.gpsimd.tensor_scalar(
-                out=bracket[:], in0=tanh_half[:], scalar1=dot_terms[i][:], scalar2=cw_half[:],
-                op0=ALU.mult, op1=ALU.add,
-            )
-            sinh2 = small.tile([P, 1], F32)
-            nc.gpsimd.tensor_scalar(
-                out=sinh2[:], in0=exp_r[:], scalar1=EXP_20, scalar2=exp_mr[:],
-                op0=ALU.min, op1=ALU.subtract,
-            )
-            gain = small.tile([P, 1], F32)
-            nc.gpsimd.tensor_scalar(
-                out=gain[:], in0=sinh2[:], scalar1=norm[:, 1:2], scalar2=bracket[:],
-                op0=ALU.mult, op1=ALU.mult,
-            )
-            gains[i] = gain
+        def scalar_product(name, in_, scale, bias=None):
+            product = small.tile([P, 1], F32, name=name, tag=name)
+            if bias is None:
+                nc.scalar.activation(out=product[:], in_=in_, func=ACT.Identity, scale=scale)
+            else:
+                nc.scalar.activation(
+                    out=product[:], in_=in_, func=ACT.Identity, scale=scale, bias=bias
+                )
+            return product
+
+        def gain_step(i, step):
+            r = norms[i][:, 0:1]
+            inv = norms[i][:, 1:2]
+            if step == 0:
+                tanh_half = small.tile([P, 1], F32)
+                exp_minus = small.tile([P, 1], F32)
+                exp_plus = small.tile([P, 1], F32)
+                nc.scalar.activation(out=tanh_half[:], in_=r, func=ACT.Tanh, scale=0.5)
+                nc.scalar.activation(out=exp_minus[:], in_=r, func=ACT.Exp, scale=-1.0)
+                nc.scalar.activation(out=exp_plus[:], in_=r, func=ACT.Exp)
+                inv_sc = scalar_product("inv_sc", inv, sc_half[:])
+                parts[i] = [tanh_half, exp_minus, exp_plus, inv_sc]
+            elif step == 1:
+                tanh_half, exp_minus, exp_plus, inv_sc = parts[i]
+                dot_term = scalar_product("dot_term", dots[i][:], inv_sc[:])
+                sinh_twice = scalar_product("sinh_twice", exp_minus[:], -1.0, exp_plus[:])
+                parts[i] = [tanh_half, dot_term, sinh_twice]
+            elif step == 2:
+                tanh_half, dot_term, sinh_twice = parts[i]
+                bracket = scalar_product("bracket", tanh_half[:], dot_term[:], cw_half[:])
+                quotient = scalar_product("quotient", sinh_twice[:], inv)
+                parts[i] = [bracket, quotient]
+            else:
+                bracket, quotient = parts[i]
+                gains[i] = scalar_product("gain", quotient[:], bracket[:])
 
         def finish(i):
             rows = slice(i * P, (i + 1) * P)
@@ -328,18 +357,29 @@ def tile_pvfc_kernel(tc, x, W_words, W_scales, b, out):
             )
             nc.sync.dma_start(out=out[rows, early], in_=result[i][:, early])
 
-        scale_rows(0)
         for k in range(LEAD):
+            square_sum(k + 2)
+            logarithm(k + 1)
+            roots(k + 2)
             quantise_rows(k)
+        logarithm(LEAD + 1)
         for i in range(ROW_TILES + 1):
             if i < ROW_TILES:
                 multiply(i)
                 sums_early(i)
             if i > 0:
-                end_gain(i - 1)
+                gain_step(i - 1, 0)
             if i < ROW_TILES:
-                sums_late(i)
-                start_gain(i)
+                sums_late(i, EARLY)
+            if i > 0:
+                gain_step(i - 1, 1)
+            if i < ROW_TILES:
+                sums_late(i, EARLY + 1)
+            if i > 0:
+                gain_step(i - 1, 2)
+                gain_step(i - 1, 3)
+            if i < ROW_TILES:
+                norm_of(i)
             if i + LEAD < ROW_TILES:
                 quantise_rows(i + LEAD)
             if i > 0:

@@ -20,7 +20,6 @@ PASSES = K // (4 * P)
 BANK = 512
 BANKS = N // BANK
 EARLY = 2
-LEAD = ROW_TILES - 2
 FLOPS = 2 * M * K * N
 
 LOG2_E = 1.4426950408889634
@@ -33,18 +32,18 @@ def tile_pvfc_kernel(tc, x, W_words, W_scales, b, out):
         ctx.enter_context(tc.manual_schedule())
         keep = ctx.enter_context(tc.tile_pool(name="keep", bufs=1))
         work = ctx.enter_context(tc.tile_pool(name="work", bufs=2))
+        scaled = ctx.enter_context(tc.tile_pool(name="scaled", bufs=3))
         scrap = ctx.enter_context(tc.tile_pool(name="scrap", bufs=4))
         small = ctx.enter_context(tc.tile_pool(name="small", bufs=3))
-        results = ctx.enter_context(tc.tile_pool(name="results", bufs=4))
-        psum_t = ctx.enter_context(tc.psum_pool(name="psum_t", bufs=2))
-        psum_early = ctx.enter_context(tc.psum_pool(name="psum_early", bufs=2))
-        psum_late = ctx.enter_context(tc.psum_pool(name="psum_late", bufs=4))
+        results = ctx.enter_context(tc.tile_pool(name="results", bufs=5))
+        psum_early = ctx.enter_context(tc.psum_pool(name="psum_early", bufs=EARLY))
+        psum_late = ctx.enter_context(tc.psum_pool(name="psum_late", bufs=2 * (BANKS - EARLY)))
 
         def constant(name, values):
-            tile = keep.tile([P, len(values)], F32, name=name)
+            columns = keep.tile([P, len(values)], F32, name=name)
             for c, value in enumerate(values):
-                nc.vector.memset(tile[:, c : c + 1], value)
-            return tile
+                nc.vector.memset(columns[:, c : c + 1], value)
+            return columns
 
         b_row = keep.tile([P, N], BF16)
         nc.vector.memset(b_row[:].bitcast(I32), 0)
@@ -89,6 +88,10 @@ def tile_pvfc_kernel(tc, x, W_words, W_scales, b, out):
 
         v_codes = keep.tile([P, ROW_TILES, PASSES * P], U32, align_bytes=64)
         v_planes = keep.tile([P, ROW_TILES, PASSES * P], U8, align_bytes=64)
+        b_bc = keep.tile([P, N], BF16)
+        sc_b = keep.tile([P, N], F32)
+        sc_half = keep.tile([P, 1], F32)
+        cw_half = keep.tile([P, 1], F32)
 
         x_sums = {}
         x_roots = {}
@@ -122,13 +125,13 @@ def tile_pvfc_kernel(tc, x, W_words, W_scales, b, out):
         v_tiles = {}
 
         def scale_rows(k):
-            v_tiles[k] = work.tile([P, K], BF16, name="v_sb", tag="v_sb")
+            v_tiles[k] = scaled.tile([P, K], BF16, name="v_sb", tag="v_sb")
             nc.vector.tensor_scalar(
                 out=v_tiles[k][:], in0=x_sb[k][:], scalar1=asinh[k][:],
                 scalar2=x_roots[k][:, 2:3], op0=ALU.mult, op1=ALU.mult,
             )
 
-        def quantise_rows(k):
+        def quantise_rows(k, psum_t):
             v_pairs = v_tiles[k][:].bitcast(F32)
             flipped = []
             for h in range(2):
@@ -149,115 +152,105 @@ def tile_pvfc_kernel(tc, x, W_words, W_scales, b, out):
                     out=grouped_pairs[:, 2 * h : 2 * h + 2, :, :],
                     in_=flipped[h][:].rearrange("p g u m -> p g m u"),
                 )
-            if k + 1 < ROW_TILES:
-                scale_rows(k + 1)
+            if k + 3 < ROW_TILES:
+                roots(k + 3)
+            if k + 2 < ROW_TILES:
+                logarithm(k + 2)
+                scale_rows(k + 2)
             nc.vector.quantize_mx(
                 out=v_codes[:, k, :].bitcast(FP8X4), scales=v_planes[:, k, :], in_=grouped[:]
             )
 
-        square_sum(0)
-        square_sum(1)
-
-        b_squares = keep.tile([P, N // P], F32)
-        b_partial = keep.tile([P, 1], F32)
-        nc.vector.scalar_tensor_tensor(
-            out=b_squares[:], in0=b_cols[:], scalar=1.0, in1=b_cols[:],
-            op0=ALU.mult, op1=ALU.mult, accum_out=b_partial[:],
-        )
-        b_repeated = keep.tile([P, P], F32)
-        nc.vector.tensor_copy(out=b_repeated[:], in_=b_partial[:].to_broadcast([P, P]))
-        b_flipped = psum_t.tile([P, 2, 2, P], F32, name="flipped", tag="flipped")
-        nc.tensor.transpose(b_flipped[:, 0, 0, :], b_repeated[:], ident[:])
-        bb = keep.tile([P, 1], F32)
-        nc.vector.reduce_sum(out=bb[:], in_=b_flipped[:, 0, 0, :], axis=AX.X)
-
-        b_banks = []
-        for j in range(BANKS):
-            bank = psum_late.tile([P, BANK], F32, name="late", tag="late")
-            nc.tensor.matmul(
-                bank[:], lhsT=ones[:], rhs=b_row[:, j * BANK : (j + 1) * BANK],
-                start=True, stop=True,
+        def numbers_of_b(psum_t):
+            b_squares = keep.tile([P, N // P], F32)
+            b_partial = keep.tile([P, 1], F32)
+            nc.vector.scalar_tensor_tensor(
+                out=b_squares[:], in0=b_cols[:], scalar=1.0, in1=b_cols[:],
+                op0=ALU.mult, op1=ALU.mult, accum_out=b_partial[:],
             )
-            b_banks.append(bank)
-        b_bc = keep.tile([P, N], BF16)
+            b_repeated = keep.tile([P, P], F32)
+            nc.vector.tensor_copy(out=b_repeated[:], in_=b_partial[:].to_broadcast([P, P]))
+            b_flipped = psum_t.tile([P, 2, 2, P], F32, name="flipped", tag="flipped")
+            nc.tensor.transpose(b_flipped[:, 0, 0, :], b_repeated[:], ident[:])
+            bb = keep.tile([P, 1], F32)
+            nc.vector.reduce_sum(out=bb[:], in_=b_flipped[:, 0, 0, :], axis=AX.X)
 
-        def copy_b(j):
-            nc.vector.tensor_copy(out=b_bc[:, j * BANK : (j + 1) * BANK], in_=b_banks[j][:])
+            b_banks = []
+            for j in range(BANKS):
+                bank = psum_late.tile([P, BANK], F32, name="late", tag="late")
+                nc.tensor.matmul(
+                    bank[:], lhsT=ones[:], rhs=b_row[:, j * BANK : (j + 1) * BANK],
+                    start=True, stop=True,
+                )
+                b_banks.append(bank)
 
-        z_radicands = keep.tile([P, 2], F32)
-        nc.vector.scalar_tensor_tensor(
-            out=z_radicands[:], in0=b_floor[:], scalar=bb[:], in1=b_cap[:],
-            op0=ALU.max, op1=ALU.min,
-        )
-        z_roots = keep.tile([P, 2], F32)
-        nc.gpsimd.tensor_tensor(
-            out=z_roots[:], in0=z_radicands[:], in1=exponents[:, 1:3], op=ALU.pow
-        )
-        copy_b(0)
-        copy_b(1)
-        z_log2e = keep.tile([P, 2], F32)
-        nc.vector.tensor_scalar_mul(z_log2e[:], z_roots[:, 0:1].to_broadcast([P, 2]), LOG2_E)
-        z_exps = keep.tile([P, 2], F32)
-        nc.gpsimd.tensor_tensor(out=z_exps[:], in0=twos[:], in1=z_log2e[:], op=ALU.pow)
-        copy_b(2)
-        copy_b(3)
-        roots(0)
-        logarithm(0)
-        sc_twice = keep.tile([P, 1], F32)
-        nc.vector.tensor_sub(sc_twice[:], z_exps[:, 0:1], z_exps[:, 1:2])
-        nc.vector.tensor_scalar(
-            out=sc_twice[:], in0=sc_twice[:], scalar1=z_roots[:, 1:2], scalar2=2.0,
-            op0=ALU.mult, op1=ALU.max,
-        )
-        sc_half = keep.tile([P, 1], F32)
-        nc.vector.tensor_scalar_mul(sc_half[:], sc_twice[:], 0.25)
-        cw_radicand = keep.tile([P, 1], F32)
-        nc.vector.tensor_mul(cw_radicand[:], sc_half[:], sc_half[:])
-        nc.vector.tensor_scalar(
-            out=cw_radicand[:], in0=cw_radicand[:], scalar1=bb[:], scalar2=0.25,
-            op0=ALU.mult, op1=ALU.add,
-        )
-        cw_half = keep.tile([P, 1], F32)
-        nc.gpsimd.tensor_tensor(
-            out=cw_half[:], in0=cw_radicand[:], in1=exponents[:, 0:1], op=ALU.pow
-        )
-        sc_b = keep.tile([P, N], F32)
-        nc.vector.tensor_scalar(
-            out=sc_b[:], in0=b_bc[:], scalar1=sc_twice[:], scalar2=0.5,
-            op0=ALU.mult, op1=ALU.mult,
-        )
-        scale_rows(0)
-        roots(1)
+            def copy_b(j):
+                nc.vector.tensor_copy(out=b_bc[:, j * BANK : (j + 1) * BANK], in_=b_banks[j][:])
+
+            z_radicands = keep.tile([P, 2], F32)
+            nc.vector.scalar_tensor_tensor(
+                out=z_radicands[:], in0=b_floor[:], scalar=bb[:], in1=b_cap[:],
+                op0=ALU.max, op1=ALU.min,
+            )
+            z_roots = keep.tile([P, 2], F32)
+            nc.gpsimd.tensor_tensor(
+                out=z_roots[:], in0=z_radicands[:], in1=exponents[:, 1:3], op=ALU.pow
+            )
+            copy_b(0)
+            copy_b(1)
+            z_log2e = keep.tile([P, 2], F32)
+            nc.vector.tensor_scalar_mul(z_log2e[:], z_roots[:, 0:1].to_broadcast([P, 2]), LOG2_E)
+            z_exps = keep.tile([P, 2], F32)
+            nc.gpsimd.tensor_tensor(out=z_exps[:], in0=twos[:], in1=z_log2e[:], op=ALU.pow)
+            copy_b(2)
+            copy_b(3)
+            roots(0)
+            logarithm(0)
+            sc_twice = keep.tile([P, 1], F32)
+            nc.vector.tensor_sub(sc_twice[:], z_exps[:, 0:1], z_exps[:, 1:2])
+            nc.vector.tensor_scalar(
+                out=sc_twice[:], in0=sc_twice[:], scalar1=z_roots[:, 1:2], scalar2=2.0,
+                op0=ALU.mult, op1=ALU.max,
+            )
+            nc.vector.tensor_scalar_mul(sc_half[:], sc_twice[:], 0.25)
+            cw_radicand = keep.tile([P, 1], F32)
+            nc.vector.tensor_mul(cw_radicand[:], sc_half[:], sc_half[:])
+            nc.vector.tensor_scalar(
+                out=cw_radicand[:], in0=cw_radicand[:], scalar1=bb[:], scalar2=0.25,
+                op0=ALU.mult, op1=ALU.add,
+            )
+            nc.gpsimd.tensor_tensor(
+                out=cw_half[:], in0=cw_radicand[:], in1=exponents[:, 0:1], op=ALU.pow
+            )
+            nc.vector.tensor_scalar(
+                out=sc_b[:], in0=b_bc[:], scalar1=sc_twice[:], scalar2=0.5,
+                op0=ALU.mult, op1=ALU.mult,
+            )
 
         banks = {}
         result = {}
         square_sums = {}
         dot_sums = {}
-        dots = {}
-        norms = {}
-        parts = {}
-        gains = {}
+        late_pools = [psum_late, psum_late]
 
-        def multiply(i):
-            banks[i] = []
-            for j in range(BANKS):
-                cols = slice(j * BANK, (j + 1) * BANK)
-                if j < EARLY:
-                    bank = psum_early.tile([P, BANK], F32, name="early", tag="early")
-                else:
-                    bank = psum_late.tile([P, BANK], F32, name="late", tag="late")
-                for g in range(PASSES):
-                    rows = slice(g * P, (g + 1) * P)
-                    nc.tensor.matmul_mx(
-                        out=bank[:],
-                        lhsT=v_codes[:, i, rows].bitcast(FP8X4),
-                        lhsT_scale=v_planes[:, i, rows],
-                        rhs=w_words[:, j, g, :].bitcast(FP8X4),
-                        rhs_scale=w_planes[4 * g : P, cols],
-                        start=(g == 0),
-                        stop=(g == PASSES - 1),
-                    )
-                banks[i].append(bank)
+        def multiply(i, j):
+            cols = slice(j * BANK, (j + 1) * BANK)
+            if j < EARLY:
+                bank = psum_early.tile([P, BANK], F32, name="early", tag="early")
+            else:
+                bank = late_pools[i % len(late_pools)].tile([P, BANK], F32, name="late", tag="late")
+            for g in range(PASSES):
+                rows = slice(g * P, (g + 1) * P)
+                nc.tensor.matmul_mx(
+                    out=bank[:],
+                    lhsT=v_codes[:, i, rows].bitcast(FP8X4),
+                    lhsT_scale=v_planes[:, i, rows],
+                    rhs=w_words[:, j, g, :].bitcast(FP8X4),
+                    rhs_scale=w_planes[4 * g : P, cols],
+                    start=(g == 0),
+                    stop=(g == PASSES - 1),
+                )
+            banks[i].append(bank)
 
         def square_sum_of_bank(i, j):
             square = scrap.tile([P, BANK], BF16)
@@ -289,6 +282,18 @@ def tile_pvfc_kernel(tc, x, W_words, W_scales, b, out):
                 accum_out=dot_sums[i][:, j - EARLY + 1 : j - EARLY + 2],
             )
 
+        norms = {}
+        dots = {}
+        tanh_half = {}
+        exp_minus = {}
+        exp_plus = {}
+        inv_sc = {}
+        dot_term = {}
+        sinh_twice = {}
+        bracket = {}
+        quotient = {}
+        gains = {}
+
         def norm_of(i):
             u_sum = small.tile([P, 1], F32)
             nc.vector.reduce_sum(out=u_sum[:], in_=square_sums[i][:], axis=AX.X)
@@ -304,41 +309,43 @@ def tile_pvfc_kernel(tc, x, W_words, W_scales, b, out):
                 out=norms[i][:], in0=radicands[:], in1=exponents[:, 1:3], op=ALU.pow
             )
 
-        def scalar_product(name, in_, scale, bias=None):
-            product = small.tile([P, 1], F32, name=name, tag=name)
-            if bias is None:
-                nc.scalar.activation(out=product[:], in_=in_, func=ACT.Identity, scale=scale)
-            else:
-                nc.scalar.activation(
-                    out=product[:], in_=in_, func=ACT.Identity, scale=scale, bias=bias
-                )
-            return product
+        def function_of_r(name, i, func, scale):
+            value = small.tile([P, 1], F32, name=name, tag=name)
+            nc.scalar.activation(out=value[:], in_=norms[i][:, 0:1], func=func, scale=scale)
+            return value
 
-        def gain_step(i, step):
-            r = norms[i][:, 0:1]
-            inv = norms[i][:, 1:2]
-            if step == 0:
-                tanh_half = small.tile([P, 1], F32)
-                exp_minus = small.tile([P, 1], F32)
-                exp_plus = small.tile([P, 1], F32)
-                nc.scalar.activation(out=tanh_half[:], in_=r, func=ACT.Tanh, scale=0.5)
-                nc.scalar.activation(out=exp_minus[:], in_=r, func=ACT.Exp, scale=-1.0)
-                nc.scalar.activation(out=exp_plus[:], in_=r, func=ACT.Exp)
-                inv_sc = scalar_product("inv_sc", inv, sc_half[:])
-                parts[i] = [tanh_half, exp_minus, exp_plus, inv_sc]
-            elif step == 1:
-                tanh_half, exp_minus, exp_plus, inv_sc = parts[i]
-                dot_term = scalar_product("dot_term", dots[i][:], inv_sc[:])
-                sinh_twice = scalar_product("sinh_twice", exp_minus[:], -1.0, exp_plus[:])
-                parts[i] = [tanh_half, dot_term, sinh_twice]
-            elif step == 2:
-                tanh_half, dot_term, sinh_twice = parts[i]
-                bracket = scalar_product("bracket", tanh_half[:], dot_term[:], cw_half[:])
-                quotient = scalar_product("quotient", sinh_twice[:], inv)
-                parts[i] = [bracket, quotient]
-            else:
-                bracket, quotient = parts[i]
-                gains[i] = scalar_product("gain", quotient[:], bracket[:])
+        def product_on_scalar(name, in_, scale):
+            value = small.tile([P, 1], F32, name=name, tag=name)
+            nc.scalar.activation(out=value[:], in_=in_, func=ACT.Identity, scale=scale)
+            return value
+
+        def product_and_sum_on_scalar(name, in_, scale, bias):
+            value = small.tile([P, 1], F32, name=name, tag=name)
+            nc.scalar.activation(
+                out=value[:], in_=in_, func=ACT.Identity, scale=scale, bias=bias
+            )
+            return value
+
+        def gain_step_1(i):
+            tanh_half[i] = function_of_r("tanh_half", i, ACT.Tanh, 0.5)
+            exp_minus[i] = function_of_r("exp_minus", i, ACT.Exp, -1.0)
+            exp_plus[i] = function_of_r("exp_plus", i, ACT.Exp, 1.0)
+            inv_sc[i] = product_on_scalar("inv_sc", norms[i][:, 1:2], sc_half[:])
+
+        def gain_step_2(i):
+            dot_term[i] = product_on_scalar("dot_term", dots[i][:], inv_sc[i][:])
+            sinh_twice[i] = product_and_sum_on_scalar(
+                "sinh_twice", exp_minus[i][:], -1.0, exp_plus[i][:]
+            )
+
+        def gain_step_3(i):
+            bracket[i] = product_and_sum_on_scalar(
+                "bracket", tanh_half[i][:], dot_term[i][:], cw_half[:]
+            )
+            quotient[i] = product_on_scalar("quotient", sinh_twice[i][:], norms[i][:, 1:2])
+
+        def gain_step_4(i):
+            gains[i] = product_on_scalar("gain", quotient[i][:], bracket[i][:])
 
         def finish(i):
             rows = slice(i * P, (i + 1) * P)
@@ -357,30 +364,44 @@ def tile_pvfc_kernel(tc, x, W_words, W_scales, b, out):
             )
             nc.sync.dma_start(out=out[rows, early], in_=result[i][:, early])
 
-        for k in range(LEAD):
-            square_sum(k + 2)
-            logarithm(k + 1)
-            roots(k + 2)
-            quantise_rows(k)
-        logarithm(LEAD + 1)
+        for i in range(ROW_TILES):
+            banks[i] = []
+        with tc.psum_pool(name="psum_t", bufs=2) as psum_t:
+            square_sum(0)
+            square_sum(1)
+            numbers_of_b(psum_t)
+            scale_rows(0)
+            roots(1)
+            square_sum(2)
+            logarithm(1)
+            roots(2)
+            scale_rows(1)
+            for k in range(ROW_TILES):
+                if k + 3 < ROW_TILES:
+                    square_sum(k + 3)
+                quantise_rows(k, psum_t)
+                if k >= ROW_TILES - BANKS:
+                    multiply(0, k - (ROW_TILES - BANKS))
+
+        late_pools.append(ctx.enter_context(tc.psum_pool(name="psum_late_2", bufs=BANKS - EARLY)))
         for i in range(ROW_TILES + 1):
+            if 0 < i < ROW_TILES:
+                for j in range(BANKS):
+                    multiply(i, j)
             if i < ROW_TILES:
-                multiply(i)
                 sums_early(i)
             if i > 0:
-                gain_step(i - 1, 0)
+                gain_step_1(i - 1)
             if i < ROW_TILES:
                 sums_late(i, EARLY)
             if i > 0:
-                gain_step(i - 1, 1)
+                gain_step_2(i - 1)
             if i < ROW_TILES:
                 sums_late(i, EARLY + 1)
             if i > 0:
-                gain_step(i - 1, 2)
-                gain_step(i - 1, 3)
+                gain_step_3(i - 1)
+                gain_step_4(i - 1)
             if i < ROW_TILES:
                 norm_of(i)
-            if i + LEAD < ROW_TILES:
-                quantise_rows(i + LEAD)
             if i > 0:
                 finish(i - 1)

@@ -20,6 +20,7 @@ PASSES = K // (4 * P)
 BANK = 512
 BANKS = N // BANK
 EARLY = 2
+FIRST_BANK_ROUND = 2
 FLOPS = 2 * M * K * N
 
 LOG2_E = 1.4426950408889634
@@ -73,10 +74,10 @@ def tile_pvfc_kernel(tc, x, W_words, W_scales, b, out):
         nc.sync.dma_start(out=b_row[0:1, :], in_=b.rearrange("(o n) -> o n", o=1))
         for i in range(1, ROW_TILES):
             nc.sync.dma_start(out=x_sb[i][:], in_=x[i * P : (i + 1) * P, :])
-        for q in range(4):
+        for quadrant in range(4):
             nc.sync.dma_start(
-                out=w_planes[32 * q : 32 * q + 16, :].bitcast(I32),
-                in_=W_scales[:, 4 * q : 4 * q + 4, :].bitcast(I32),
+                out=w_planes[32 * quadrant : 32 * quadrant + 16, :].bitcast(I32),
+                in_=W_scales[:, 4 * quadrant : 4 * quadrant + 4, :].bitcast(I32),
             )
         w_words = keep.tile([P, BANKS, PASSES, BANK], U32, align_bytes=64)
         w_view = W_words.rearrange("g p n t -> p g (n t)").bitcast(I32)
@@ -124,15 +125,15 @@ def tile_pvfc_kernel(tc, x, W_words, W_scales, b, out):
 
         v_tiles = {}
 
-        def scale_rows(k):
-            v_tiles[k] = scaled.tile([P, K], BF16, name="v_sb", tag="v_sb")
+        def scale_rows(i):
+            v_tiles[i] = scaled.tile([P, K], BF16, name="v_sb", tag="v_sb")
             nc.vector.tensor_scalar(
-                out=v_tiles[k][:], in0=x_sb[k][:], scalar1=asinh[k][:],
-                scalar2=x_roots[k][:, 2:3], op0=ALU.mult, op1=ALU.mult,
+                out=v_tiles[i][:], in0=x_sb[i][:], scalar1=asinh[i][:],
+                scalar2=x_roots[i][:, 2:3], op0=ALU.mult, op1=ALU.mult,
             )
 
-        def quantise_rows(k, psum_t):
-            v_pairs = v_tiles[k][:].bitcast(F32)
+        def quantise_rows(i, psum_t):
+            v_pairs = v_tiles[i][:].bitcast(F32)
             flipped = []
             for h in range(2):
                 bank = psum_t.tile([P, 2, 2, P], F32, name="flipped", tag="flipped")
@@ -152,16 +153,24 @@ def tile_pvfc_kernel(tc, x, W_words, W_scales, b, out):
                     out=grouped_pairs[:, 2 * h : 2 * h + 2, :, :],
                     in_=flipped[h][:].rearrange("p g u m -> p g m u"),
                 )
-            if k + 3 < ROW_TILES:
-                roots(k + 3)
-            if k + 2 < ROW_TILES:
-                logarithm(k + 2)
-                scale_rows(k + 2)
+            if i + 3 < ROW_TILES:
+                roots(i + 3)
+            if i + 2 < ROW_TILES:
+                logarithm(i + 2)
+                scale_rows(i + 2)
             nc.vector.quantize_mx(
-                out=v_codes[:, k, :].bitcast(FP8X4), scales=v_planes[:, k, :], in_=grouped[:]
+                out=v_codes[:, i, :].bitcast(FP8X4), scales=v_planes[:, i, :], in_=grouped[:]
             )
 
-        def numbers_of_b(psum_t):
+        b_banks = []
+        bb = keep.tile([P, 1], F32)
+        z_roots = keep.tile([P, 2], F32)
+        z_exps = keep.tile([P, 2], F32)
+
+        def copy_b(j):
+            nc.vector.tensor_copy(out=b_bc[:, j * BANK : (j + 1) * BANK], in_=b_banks[j][:])
+
+        def numbers_of_b_1(psum_t):
             b_squares = keep.tile([P, N // P], F32)
             b_partial = keep.tile([P, 1], F32)
             nc.vector.scalar_tensor_tensor(
@@ -172,10 +181,8 @@ def tile_pvfc_kernel(tc, x, W_words, W_scales, b, out):
             nc.vector.tensor_copy(out=b_repeated[:], in_=b_partial[:].to_broadcast([P, P]))
             b_flipped = psum_t.tile([P, 2, 2, P], F32, name="flipped", tag="flipped")
             nc.tensor.transpose(b_flipped[:, 0, 0, :], b_repeated[:], ident[:])
-            bb = keep.tile([P, 1], F32)
             nc.vector.reduce_sum(out=bb[:], in_=b_flipped[:, 0, 0, :], axis=AX.X)
 
-            b_banks = []
             for j in range(BANKS):
                 bank = psum_late.tile([P, BANK], F32, name="late", tag="late")
                 nc.tensor.matmul(
@@ -184,28 +191,25 @@ def tile_pvfc_kernel(tc, x, W_words, W_scales, b, out):
                 )
                 b_banks.append(bank)
 
-            def copy_b(j):
-                nc.vector.tensor_copy(out=b_bc[:, j * BANK : (j + 1) * BANK], in_=b_banks[j][:])
-
             z_radicands = keep.tile([P, 2], F32)
             nc.vector.scalar_tensor_tensor(
                 out=z_radicands[:], in0=b_floor[:], scalar=bb[:], in1=b_cap[:],
                 op0=ALU.max, op1=ALU.min,
             )
-            z_roots = keep.tile([P, 2], F32)
             nc.gpsimd.tensor_tensor(
                 out=z_roots[:], in0=z_radicands[:], in1=exponents[:, 1:3], op=ALU.pow
             )
             copy_b(0)
             copy_b(1)
+
+        def numbers_of_b_2():
             z_log2e = keep.tile([P, 2], F32)
             nc.vector.tensor_scalar_mul(z_log2e[:], z_roots[:, 0:1].to_broadcast([P, 2]), LOG2_E)
-            z_exps = keep.tile([P, 2], F32)
             nc.gpsimd.tensor_tensor(out=z_exps[:], in0=twos[:], in1=z_log2e[:], op=ALU.pow)
             copy_b(2)
             copy_b(3)
-            roots(0)
-            logarithm(0)
+
+        def numbers_of_b_3():
             sc_twice = keep.tile([P, 1], F32)
             nc.vector.tensor_sub(sc_twice[:], z_exps[:, 0:1], z_exps[:, 1:2])
             nc.vector.tensor_scalar(
@@ -240,11 +244,11 @@ def tile_pvfc_kernel(tc, x, W_words, W_scales, b, out):
             else:
                 bank = late_pools[i % len(late_pools)].tile([P, BANK], F32, name="late", tag="late")
             for g in range(PASSES):
-                rows = slice(g * P, (g + 1) * P)
+                words = slice(g * P, (g + 1) * P)
                 nc.tensor.matmul_mx(
                     out=bank[:],
-                    lhsT=v_codes[:, i, rows].bitcast(FP8X4),
-                    lhsT_scale=v_planes[:, i, rows],
+                    lhsT=v_codes[:, i, words].bitcast(FP8X4),
+                    lhsT_scale=v_planes[:, i, words],
                     rhs=w_words[:, j, g, :].bitcast(FP8X4),
                     rhs_scale=w_planes[4 * g : P, cols],
                     start=(g == 0),
@@ -369,19 +373,23 @@ def tile_pvfc_kernel(tc, x, W_words, W_scales, b, out):
         with tc.psum_pool(name="psum_t", bufs=2) as psum_t:
             square_sum(0)
             square_sum(1)
-            numbers_of_b(psum_t)
+            numbers_of_b_1(psum_t)
+            roots(0)
+            logarithm(0)
+            numbers_of_b_2()
             scale_rows(0)
             roots(1)
             square_sum(2)
             logarithm(1)
-            roots(2)
+            numbers_of_b_3()
             scale_rows(1)
-            for k in range(ROW_TILES):
-                if k + 3 < ROW_TILES:
-                    square_sum(k + 3)
-                quantise_rows(k, psum_t)
-                if k >= ROW_TILES - BANKS:
-                    multiply(0, k - (ROW_TILES - BANKS))
+            roots(2)
+            for i in range(ROW_TILES):
+                if i + 3 < ROW_TILES:
+                    square_sum(i + 3)
+                quantise_rows(i, psum_t)
+                if FIRST_BANK_ROUND <= i < FIRST_BANK_ROUND + BANKS:
+                    multiply(0, i - FIRST_BANK_ROUND)
 
         late_pools.append(ctx.enter_context(tc.psum_pool(name="psum_late_2", bufs=BANKS - EARLY)))
         for i in range(ROW_TILES + 1):

@@ -20,7 +20,7 @@ PASSES = K // (4 * P)
 BANK = 512
 BANKS = N // BANK
 EARLY = 2
-FIRST_BANK_ROUND = 2
+LAG = 4
 FLOPS = 2 * M * K * N
 
 LOG2_E = 1.4426950408889634
@@ -149,10 +149,16 @@ def tile_pvfc_kernel(tc, x, W_words, W_scales, b, out):
                 "p (g m u) -> p g m u", g=PASSES, u=2
             )
             for h in range(2):
-                nc.vector.tensor_copy(
-                    out=grouped_pairs[:, 2 * h : 2 * h + 2, :, :],
-                    in_=flipped[h][:].rearrange("p g u m -> p g m u"),
-                )
+                if i >= 3:
+                    nc.scalar.copy(
+                        out=grouped_pairs[:, 2 * h : 2 * h + 2, :, :],
+                        in_=flipped[h][:].rearrange("p g u m -> p g m u"),
+                    )
+                else:
+                    nc.vector.tensor_copy(
+                        out=grouped_pairs[:, 2 * h : 2 * h + 2, :, :],
+                        in_=flipped[h][:].rearrange("p g u m -> p g m u"),
+                    )
             if i + 3 < ROW_TILES:
                 roots(i + 3)
             if i + 2 < ROW_TILES:
@@ -368,6 +374,27 @@ def tile_pvfc_kernel(tc, x, W_words, W_scales, b, out):
             )
             nc.sync.dma_start(out=out[rows, early], in_=result[i][:, early])
 
+        def second_phase_round(i):
+            if 0 <= i < ROW_TILES:
+                for j in range(BANKS):
+                    multiply(i, j)
+                sums_early(i)
+            if 0 < i <= ROW_TILES:
+                gain_step_1(i - 1)
+            if 0 <= i < ROW_TILES:
+                sums_late(i, EARLY)
+            if 0 < i <= ROW_TILES:
+                gain_step_2(i - 1)
+            if 0 <= i < ROW_TILES:
+                sums_late(i, EARLY + 1)
+            if 0 < i <= ROW_TILES:
+                gain_step_3(i - 1)
+                gain_step_4(i - 1)
+            if 0 <= i < ROW_TILES:
+                norm_of(i)
+            if 0 < i <= ROW_TILES:
+                finish(i - 1)
+
         for i in range(ROW_TILES):
             banks[i] = []
         with tc.psum_pool(name="psum_t", bufs=2) as psum_t:
@@ -388,28 +415,7 @@ def tile_pvfc_kernel(tc, x, W_words, W_scales, b, out):
                 if i + 3 < ROW_TILES:
                     square_sum(i + 3)
                 quantise_rows(i, psum_t)
-                if FIRST_BANK_ROUND <= i < FIRST_BANK_ROUND + BANKS:
-                    multiply(0, i - FIRST_BANK_ROUND)
-
+                second_phase_round(i - LAG)
         late_pools.append(ctx.enter_context(tc.psum_pool(name="psum_late_2", bufs=BANKS - EARLY)))
-        for i in range(ROW_TILES + 1):
-            if 0 < i < ROW_TILES:
-                for j in range(BANKS):
-                    multiply(i, j)
-            if i < ROW_TILES:
-                sums_early(i)
-            if i > 0:
-                gain_step_1(i - 1)
-            if i < ROW_TILES:
-                sums_late(i, EARLY)
-            if i > 0:
-                gain_step_2(i - 1)
-            if i < ROW_TILES:
-                sums_late(i, EARLY + 1)
-            if i > 0:
-                gain_step_3(i - 1)
-                gain_step_4(i - 1)
-            if i < ROW_TILES:
-                norm_of(i)
-            if i > 0:
-                finish(i - 1)
+        for i in range(ROW_TILES, ROW_TILES + LAG + 1):
+            second_phase_round(i - LAG)

@@ -149,7 +149,7 @@ def tile_pvfc_kernel(tc, x, W_words, W_scales, b, out):
                 "p (g m u) -> p g m u", g=PASSES, u=2
             )
             for h in range(2):
-                if i >= 3:
+                if i >= 5:
                     nc.scalar.copy(
                         out=grouped_pairs[:, 2 * h : 2 * h + 2, :, :],
                         in_=flipped[h][:].rearrange("p g u m -> p g m u"),

@@ -21,6 +21,7 @@ BANK = 512
 BANKS = N // BANK
 EARLY = 2
 LAG = 4
+WARM_UP = 4
 FLOPS = 2 * M * K * N
 
 LOG2_E = 1.4426950408889634
@@ -374,6 +375,11 @@ def tile_pvfc_kernel(tc, x, W_words, W_scales, b, out):
             )
             nc.sync.dma_start(out=out[rows, early], in_=result[i][:, early])
 
+        def warm_up():
+            idle = psum_late.tile([P, BANK], F32, name="late", tag="late")
+            for repeat in range(WARM_UP):
+                nc.tensor.matmul(idle[:], lhsT=ones[:], rhs=b_row[:, 0:BANK], start=True, stop=True)
+
         def second_phase_round(i):
             if 0 <= i < ROW_TILES:
                 for j in range(BANKS):
@@ -415,6 +421,8 @@ def tile_pvfc_kernel(tc, x, W_words, W_scales, b, out):
                 if i + 3 < ROW_TILES:
                     square_sum(i + 3)
                 quantise_rows(i, psum_t)
+                if i == LAG - 1:
+                    warm_up()
                 second_phase_round(i - LAG)
         late_pools.append(ctx.enter_context(tc.psum_pool(name="psum_late_2", bufs=BANKS - EARLY)))
         for i in range(ROW_TILES, ROW_TILES + LAG + 1):

@@ -421,7 +421,7 @@ def tile_pvfc_kernel(tc, x, W_words, W_scales, b, out):
                 if i + 3 < ROW_TILES:
                     square_sum(i + 3)
                 quantise_rows(i, psum_t)
-                if i == LAG - 1:
+                if i < LAG:
                     warm_up()
                 second_phase_round(i - LAG)
         late_pools.append(ctx.enter_context(tc.psum_pool(name="psum_late_2", bufs=BANKS - EARLY)))

@@ -410,6 +410,7 @@ def tile_pvfc_kernel(tc, x, W_words, W_scales, b, out):
             roots(0)
             logarithm(0)
             numbers_of_b_2()
+            warm_up()
             scale_rows(0)
             roots(1)
             square_sum(2)

from contextlib import ExitStack

import concourse.mybir as mybir
from concourse.masks import make_identity

F32 = mybir.dt.float32
BF16 = mybir.dt.bfloat16
I32 = mybir.dt.int32
U32 = mybir.dt.uint32
U8 = mybir.dt.uint8
FP8X4 = mybir.dt.float8_e4m3fn_x4
ALU = mybir.AluOpType
ACT = mybir.ActivationFunctionType
AX = mybir.AxisListType

P = 128
M, K, N = 1024, 2048, 2048
ROW_TILES = M // P
PASSES = K // (4 * P)
BANK = 512
BANKS = N // BANK
EARLY = 2
LAG = 4
WARM_UP = 4
FLOPS = 2 * M * K * N

LOG2_E = 1.4426950408889634
HUGE = 3.0e38


def tile_pvfc_kernel(tc, x, W_words, W_scales, b, out):
    nc = tc.nc
    with ExitStack() as ctx:
        ctx.enter_context(tc.manual_schedule())
        keep = ctx.enter_context(tc.tile_pool(name="keep", bufs=1))
        work = ctx.enter_context(tc.tile_pool(name="work", bufs=2))
        scaled = ctx.enter_context(tc.tile_pool(name="scaled", bufs=3))
        scrap = ctx.enter_context(tc.tile_pool(name="scrap", bufs=4))
        small = ctx.enter_context(tc.tile_pool(name="small", bufs=3))
        results = ctx.enter_context(tc.tile_pool(name="results", bufs=5))
        psum_early = ctx.enter_context(tc.psum_pool(name="psum_early", bufs=EARLY))
        psum_late = ctx.enter_context(tc.psum_pool(name="psum_late", bufs=2 * (BANKS - EARLY)))

        def constant(name, values):
            columns = keep.tile([P, len(values)], F32, name=name)
            for c, value in enumerate(values):
                nc.vector.memset(columns[:, c : c + 1], value)
            return columns

        b_row = keep.tile([P, N], BF16)
        nc.vector.memset(b_row[:].bitcast(I32), 0)
        w_planes = keep.tile([P, N], U8, align_bytes=64)
        nc.vector.memset(w_planes[:].bitcast(I32), 0)
        ones = keep.tile([P, P], BF16)
        nc.vector.memset(ones[:], 1.0)
        twos = constant("twos", [2.0, 0.5])
        exponents = constant("exponents", [0.5, 0.5, -0.5])
        b_floor = constant("b_floor", [1e-15, 1e-12])
        b_cap = constant("b_cap", [400.0, 400.0])
        x_step = constant("x_step", [0.0, 1.0, 0.0])
        x_floor = constant("x_floor", [0.0, 0.0, 1e-12])
        u_cap = constant("u_cap", [400.0, HUGE])
        u_floor = constant("u_floor", [0.0, 1e-12])
        ident = keep.tile([P, P], F32)
        make_identity(nc, ident[:])
        warm = keep.tile([P, 1], F32)
        nc.scalar.activation(out=warm[:], in_=twos[:, 0:1], func=ACT.Ln)

        x_sb = []
        for i in range(ROW_TILES):
            x_sb.append(keep.tile([P, K], BF16, name="x%d" % i))
        b_cols = keep.tile([P, N // P], BF16)
        nc.sync.dma_start(out=x_sb[0][:], in_=x[0:P, :])
        nc.sync.dma_start(out=b_cols[:], in_=b.rearrange("(p c) -> p c", p=P))
        nc.sync.dma_start(out=b_row[0:1, :], in_=b.rearrange("(o n) -> o n", o=1))
        for i in range(1, ROW_TILES):
            nc.sync.dma_start(out=x_sb[i][:], in_=x[i * P : (i + 1) * P, :])
        for quadrant in range(4):
            nc.sync.dma_start(
                out=w_planes[32 * quadrant : 32 * quadrant + 16, :].bitcast(I32),
                in_=W_scales[:, 4 * quadrant : 4 * quadrant + 4, :].bitcast(I32),
            )
        w_words = keep.tile([P, BANKS, PASSES, BANK], U32, align_bytes=64)
        w_view = W_words.rearrange("g p n t -> p g (n t)").bitcast(I32)
        for j in range(BANKS):
            nc.sync.dma_start(
                out=w_words[:, j, :, :].bitcast(I32),
                in_=w_view[:, :, j * BANK : (j + 1) * BANK],
            )

        v_codes = keep.tile([P, ROW_TILES, PASSES * P], U32, align_bytes=64)
        v_planes = keep.tile([P, ROW_TILES, PASSES * P], U8, align_bytes=64)
        b_bc = keep.tile([P, N], BF16)
        sc_b = keep.tile([P, N], F32)
        sc_half = keep.tile([P, 1], F32)
        cw_half = keep.tile([P, 1], F32)

        x_sums = {}
        x_roots = {}
        asinh = {}

        def square_sum(i):
            squares = work.tile([P, K], BF16)
            x_sums[i] = keep.tile([P, 1], F32, name="x_sum%d" % i)
            nc.scalar.activation(
                out=squares[:], in_=x_sb[i][:], func=ACT.Square, accum_out=x_sums[i][:]
            )

        def roots(i):
            radicands = keep.tile([P, 3], F32, name="radicands%d" % i)
            nc.vector.scalar_tensor_tensor(
                out=radicands[:], in0=x_step[:], scalar=x_sums[i][:], in1=x_floor[:],
                op0=ALU.add, op1=ALU.max,
            )
            x_roots[i] = keep.tile([P, 3], F32, name="x_roots%d" % i)
            nc.gpsimd.tensor_tensor(
                out=x_roots[i][:], in0=radicands[:], in1=exponents[:], op=ALU.pow
            )

        def logarithm(i):
            asinh[i] = keep.tile([P, 1], F32, name="asinh%d" % i)
            nc.scalar.activation(
                out=asinh[i][:], in_=x_roots[i][:, 0:1], func=ACT.Ln,
                bias=x_roots[i][:, 1:2], scale=1.0,
            )

        v_tiles = {}

        def scale_rows(i):
            v_tiles[i] = scaled.tile([P, K], BF16, name="v_sb", tag="v_sb")
            nc.vector.tensor_scalar(
                out=v_tiles[i][:], in0=x_sb[i][:], scalar1=asinh[i][:],
                scalar2=x_roots[i][:, 2:3], op0=ALU.mult, op1=ALU.mult,
            )

        def quantise_rows(i, psum_t):
            v_pairs = v_tiles[i][:].bitcast(F32)
            flipped = []
            for h in range(2):
                bank = psum_t.tile([P, 2, 2, P], F32, name="flipped", tag="flipped")
                for gg in range(2):
                    g = 2 * h + gg
                    for u in range(2):
                        nc.tensor.transpose(
                            bank[:, gg, u, :], v_pairs[:, 256 * g + u : 256 * (g + 1) : 2], ident[:]
                        )
                flipped.append(bank)
            grouped = work.tile([P, K], BF16, align_bytes=64)
            grouped_pairs = grouped[:].bitcast(F32).rearrange(
                "p (g m u) -> p g m u", g=PASSES, u=2
            )
            for h in range(2):
                if i >= 5:
                    nc.scalar.copy(
                        out=grouped_pairs[:, 2 * h : 2 * h + 2, :, :],
                        in_=flipped[h][:].rearrange("p g u m -> p g m u"),
                    )
                else:
                    nc.vector.tensor_copy(
                        out=grouped_pairs[:, 2 * h : 2 * h + 2, :, :],
                        in_=flipped[h][:].rearrange("p g u m -> p g m u"),
                    )
            if i + 3 < ROW_TILES:
                roots(i + 3)
            if i + 2 < ROW_TILES:
                logarithm(i + 2)
                scale_rows(i + 2)
            nc.vector.quantize_mx(
                out=v_codes[:, i, :].bitcast(FP8X4), scales=v_planes[:, i, :], in_=grouped[:]
            )

        b_banks = []
        bb = keep.tile([P, 1], F32)
        z_roots = keep.tile([P, 2], F32)
        z_exps = keep.tile([P, 2], F32)

        def copy_b(j):
            nc.vector.tensor_copy(out=b_bc[:, j * BANK : (j + 1) * BANK], in_=b_banks[j][:])

        def numbers_of_b_1(psum_t):
            b_squares = keep.tile([P, N // P], F32)
            b_partial = keep.tile([P, 1], F32)
            nc.vector.scalar_tensor_tensor(
                out=b_squares[:], in0=b_cols[:], scalar=1.0, in1=b_cols[:],
                op0=ALU.mult, op1=ALU.mult, accum_out=b_partial[:],
            )
            b_repeated = keep.tile([P, P], F32)
            nc.vector.tensor_copy(out=b_repeated[:], in_=b_partial[:].to_broadcast([P, P]))
            b_flipped = psum_t.tile([P, 2, 2, P], F32, name="flipped", tag="flipped")
            nc.tensor.transpose(b_flipped[:, 0, 0, :], b_repeated[:], ident[:])
            nc.vector.reduce_sum(out=bb[:], in_=b_flipped[:, 0, 0, :], axis=AX.X)

            for j in range(BANKS):
                bank = psum_late.tile([P, BANK], F32, name="late", tag="late")
                nc.tensor.matmul(
                    bank[:], lhsT=ones[:], rhs=b_row[:, j * BANK : (j + 1) * BANK],
                    start=True, stop=True,
                )
                b_banks.append(bank)

            z_radicands = keep.tile([P, 2], F32)
            nc.vector.scalar_tensor_tensor(
                out=z_radicands[:], in0=b_floor[:], scalar=bb[:], in1=b_cap[:],
                op0=ALU.max, op1=ALU.min,
            )
            nc.gpsimd.tensor_tensor(
                out=z_roots[:], in0=z_radicands[:], in1=exponents[:, 1:3], op=ALU.pow
            )
            copy_b(0)
            copy_b(1)

        def numbers_of_b_2():
            z_log2e = keep.tile([P, 2], F32)
            nc.vector.tensor_scalar_mul(z_log2e[:], z_roots[:, 0:1].to_broadcast([P, 2]), LOG2_E)
            nc.gpsimd.tensor_tensor(out=z_exps[:], in0=twos[:], in1=z_log2e[:], op=ALU.pow)
            copy_b(2)
            copy_b(3)

        def numbers_of_b_3():
            sc_twice = keep.tile([P, 1], F32)
            nc.vector.tensor_sub(sc_twice[:], z_exps[:, 0:1], z_exps[:, 1:2])
            nc.vector.tensor_scalar(
                out=sc_twice[:], in0=sc_twice[:], scalar1=z_roots[:, 1:2], scalar2=2.0,
                op0=ALU.mult, op1=ALU.max,
            )
            nc.vector.tensor_scalar_mul(sc_half[:], sc_twice[:], 0.25)
            cw_radicand = keep.tile([P, 1], F32)
            nc.vector.tensor_mul(cw_radicand[:], sc_half[:], sc_half[:])
            nc.vector.tensor_scalar(
                out=cw_radicand[:], in0=cw_radicand[:], scalar1=bb[:], scalar2=0.25,
                op0=ALU.mult, op1=ALU.add,
            )
            nc.gpsimd.tensor_tensor(
                out=cw_half[:], in0=cw_radicand[:], in1=exponents[:, 0:1], op=ALU.pow
            )
            nc.vector.tensor_scalar(
                out=sc_b[:], in0=b_bc[:], scalar1=sc_twice[:], scalar2=0.5,
                op0=ALU.mult, op1=ALU.mult,
            )

        banks = {}
        result = {}
        square_sums = {}
        dot_sums = {}
        late_pools = [psum_late, psum_late]

        def multiply(i, j):
            cols = slice(j * BANK, (j + 1) * BANK)
            if j < EARLY:
                bank = psum_early.tile([P, BANK], F32, name="early", tag="early")
            else:
                bank = late_pools[i % len(late_pools)].tile([P, BANK], F32, name="late", tag="late")
            for g in range(PASSES):
                words = slice(g * P, (g + 1) * P)
                nc.tensor.matmul_mx(
                    out=bank[:],
                    lhsT=v_codes[:, i, words].bitcast(FP8X4),
                    lhsT_scale=v_planes[:, i, words],
                    rhs=w_words[:, j, g, :].bitcast(FP8X4),
                    rhs_scale=w_planes[4 * g : P, cols],
                    start=(g == 0),
                    stop=(g == PASSES - 1),
                )
            banks[i].append(bank)

        def square_sum_of_bank(i, j):
            square = scrap.tile([P, BANK], BF16)
            nc.scalar.activation(
                out=square[:], in_=banks[i][j][:], func=ACT.Square,
                accum_out=square_sums[i][:, j : j + 1],
            )

        def sums_early(i):
            square_sums[i] = small.tile([P, BANKS], F32, name="square_sums", tag="square_sums")
            dot_sums[i] = small.tile([P, BANKS - EARLY + 1], F32, name="dot_sums", tag="dot_sums")
            result[i] = results.tile([P, N], F32, name="result", tag="result")
            for j in range(EARLY):
                square_sum_of_bank(i, j)
                nc.scalar.copy(out=result[i][:, j * BANK : (j + 1) * BANK], in_=banks[i][j][:])
            early = slice(0, EARLY * BANK)
            product = scrap.tile([P, EARLY * BANK], F32)
            nc.vector.scalar_tensor_tensor(
                out=product[:], in0=result[i][:, early], scalar=1.0, in1=b_bc[:, early],
                op0=ALU.mult, op1=ALU.mult, accum_out=dot_sums[i][:, 0:1],
            )

        def sums_late(i, j):
            square_sum_of_bank(i, j)
            product = scrap.tile([P, EARLY * BANK], F32)
            nc.vector.scalar_tensor_tensor(
                out=product[:, 0:BANK], in0=banks[i][j][:], scalar=1.0,
                in1=b_bc[:, j * BANK : (j + 1) * BANK], op0=ALU.mult, op1=ALU.mult,
                accum_out=dot_sums[i][:, j - EARLY + 1 : j - EARLY + 2],
            )

        norms = {}
        dots = {}
        tanh_half = {}
        exp_minus = {}
        exp_plus = {}
        inv_sc = {}
        dot_term = {}
        sinh_twice = {}
        bracket = {}
        quotient = {}
        gains = {}

        def norm_of(i):
            u_sum = small.tile([P, 1], F32)
            nc.vector.reduce_sum(out=u_sum[:], in_=square_sums[i][:], axis=AX.X)
            dots[i] = small.tile([P, 1], F32, name="dot", tag="dot")
            nc.vector.reduce_sum(out=dots[i][:], in_=dot_sums[i][:], axis=AX.X)
            radicands = small.tile([P, 2], F32)
            nc.vector.scalar_tensor_tensor(
                out=radicands[:], in0=u_cap[:], scalar=u_sum[:], in1=u_floor[:],
                op0=ALU.min, op1=ALU.max,
            )
            norms[i] = small.tile([P, 2], F32, name="norm", tag="norm")
            nc.gpsimd.tensor_tensor(
                out=norms[i][:], in0=radicands[:], in1=exponents[:, 1:3], op=ALU.pow
            )

        def function_of_r(name, i, func, scale):
            value = small.tile([P, 1], F32, name=name, tag=name)
            nc.scalar.activation(out=value[:], in_=norms[i][:, 0:1], func=func, scale=scale)
            return value

        def product_on_scalar(name, in_, scale):
            value = small.tile([P, 1], F32, name=name, tag=name)
            nc.scalar.activation(out=value[:], in_=in_, func=ACT.Identity, scale=scale)
            return value

        def product_and_sum_on_scalar(name, in_, scale, bias):
            value = small.tile([P, 1], F32, name=name, tag=name)
            nc.scalar.activation(
                out=value[:], in_=in_, func=ACT.Identity, scale=scale, bias=bias
            )
            return value

        def gain_step_1(i):
            tanh_half[i] = function_of_r("tanh_half", i, ACT.Tanh, 0.5)
            exp_minus[i] = function_of_r("exp_minus", i, ACT.Exp, -1.0)
            exp_plus[i] = function_of_r("exp_plus", i, ACT.Exp, 1.0)
            inv_sc[i] = product_on_scalar("inv_sc", norms[i][:, 1:2], sc_half[:])

        def gain_step_2(i):
            dot_term[i] = product_on_scalar("dot_term", dots[i][:], inv_sc[i][:])
            sinh_twice[i] = product_and_sum_on_scalar(
                "sinh_twice", exp_minus[i][:], -1.0, exp_plus[i][:]
            )

        def gain_step_3(i):
            bracket[i] = product_and_sum_on_scalar(
                "bracket", tanh_half[i][:], dot_term[i][:], cw_half[:]
            )
            quotient[i] = product_on_scalar("quotient", sinh_twice[i][:], norms[i][:, 1:2])

        def gain_step_4(i):
            gains[i] = product_on_scalar("gain", quotient[i][:], bracket[i][:])

        def finish(i):
            rows = slice(i * P, (i + 1) * P)
            for j in range(EARLY, BANKS):
                cols = slice(j * BANK, (j + 1) * BANK)
                nc.vector.scalar_tensor_tensor(
                    out=result[i][:, cols], in0=banks[i][j][:], scalar=gains[i][:],
                    in1=sc_b[:, cols], op0=ALU.mult, op1=ALU.add,
                )
            late = slice(EARLY * BANK, N)
            nc.sync.dma_start(out=out[rows, late], in_=result[i][:, late])
            early = slice(0, EARLY * BANK)
            nc.vector.scalar_tensor_tensor(
                out=result[i][:, early], in0=result[i][:, early], scalar=gains[i][:],
                in1=sc_b[:, early], op0=ALU.mult, op1=ALU.add,
            )
            nc.sync.dma_start(out=out[rows, early], in_=result[i][:, early])

        def warm_up():
            idle = psum_late.tile([P, BANK], F32, name="late", tag="late")
            for repeat in range(WARM_UP):
                nc.tensor.matmul(idle[:], lhsT=ones[:], rhs=b_row[:, 0:BANK], start=True, stop=True)

        def second_phase_round(i):
            if 0 <= i < ROW_TILES:
                for j in range(BANKS):
                    multiply(i, j)
                sums_early(i)
            if 0 < i <= ROW_TILES:
                gain_step_1(i - 1)
            if 0 <= i < ROW_TILES:
                sums_late(i, EARLY)
            if 0 < i <= ROW_TILES:
                gain_step_2(i - 1)
            if 0 <= i < ROW_TILES:
                sums_late(i, EARLY + 1)
            if 0 < i <= ROW_TILES:
                gain_step_3(i - 1)
                gain_step_4(i - 1)
            if 0 <= i < ROW_TILES:
                norm_of(i)
            if 0 < i <= ROW_TILES:
                finish(i - 1)

        for i in range(ROW_TILES):
            banks[i] = []
        with tc.psum_pool(name="psum_t", bufs=2) as psum_t:
            square_sum(0)
            square_sum(1)
            numbers_of_b_1(psum_t)
            roots(0)
            logarithm(0)
            numbers_of_b_2()
            warm_up()
            scale_rows(0)
            roots(1)
            square_sum(2)
            logarithm(1)
            numbers_of_b_3()
            scale_rows(1)
            roots(2)
            for i in range(ROW_TILES):
                if i + 3 < ROW_TILES:
                    square_sum(i + 3)
                quantise_rows(i, psum_t)
                if i < LAG:
                    warm_up()
                second_phase_round(i - LAG)
        late_pools.append(ctx.enter_context(tc.psum_pool(name="psum_late_2", bufs=BANKS - EARLY)))
        for i in range(ROW_TILES, ROW_TILES + LAG + 1):
            second_phase_round(i - LAG)
